import numpy as np
import ml_dtypes


def mxq(x, axis, fmt="e4m3"):
    dtype, down = {"e4m3": (ml_dtypes.float8_e4m3fn, 7), "e5m2": (ml_dtypes.float8_e5m2, 14)}[fmt]
    v = np.moveaxis(np.asarray(x, np.float32).astype(ml_dtypes.bfloat16).astype(np.float64), axis, -1)
    blocks = v.reshape(v.shape[:-1] + (-1, 32))
    amax = np.abs(blocks).max(-1, keepdims=True)
    byte = np.maximum(np.where(amax > 0, np.frexp(amax)[1] - 1 + 127, 0) - down, 1)
    scale = np.exp2(byte - 127.0)
    codes = (blocks / scale).astype(np.float32).astype(dtype).astype(np.float64)
    return np.moveaxis((codes * scale).reshape(v.shape), -1, axis)


WIDE = False


def mx_kscale(k):
    if not WIDE:
        return np.ones(k)
    levels = np.array([10, -10, 5, -5, 0])
    a = np.random.permutation(np.resize(levels, k // 512 * 4)).reshape(k // 512, 4)
    idx = np.arange(k)
    return np.exp2(a[idx // 512, idx % 128 // 32])


BF16 = ml_dtypes.bfloat16


def bf(x):
    return np.asarray(x, np.float32).astype(BF16)


def f64(x):
    return np.asarray(x).astype(np.float64)


E2M1 = np.array([0.0, 0.5, 1.0, 1.5, 2.0, 3.0, 4.0, 6.0, -0.0, -0.5, -1.0, -1.5, -2.0, -3.0, -4.0, -6.0])


def pack_weight(w, fmt):
    k, n = w.shape
    w = f64(bf(w)).reshape(k // 32, 32, n)
    amax = np.abs(w).max(1)
    if fmt == "e4m3":
        byte = np.frexp(amax)[1] - 1 + 127 - 7
    else:
        mant, ex = np.frexp(amax / 6.0)
        byte = np.where(mant > 0.5, ex, ex - 1) + 127
    byte = np.clip(np.where(amax > 0, byte, 1), 1, 254)
    scaled = (w * np.exp2(127.0 - byte)[:, None, :]).reshape(k, n).astype(np.float32)
    by_word = np.ascontiguousarray(scaled.reshape(k // 512, 128, 4, n).transpose(0, 1, 3, 2))
    if fmt == "e4m3":
        words = by_word.astype(ml_dtypes.float8_e4m3fn).view(np.uint8)
    else:
        c = by_word.astype(ml_dtypes.float4_e2m1fn).view(np.uint8) & 0xF
        words = c[..., 0::2] | (c[..., 1::2] << 4)
    return np.ascontiguousarray(words), np.ascontiguousarray(byte.astype(np.uint8).reshape(k // 512, 16, n))


def unpack_weight(words, scales, fmt):
    g, p, n, _ = words.shape
    if fmt == "e4m3":
        vals = np.ascontiguousarray(words).view(ml_dtypes.float8_e4m3fn).astype(np.float64)
    else:
        nib = np.empty((g, p, n, 4), np.uint8)
        nib[..., 0::2] = words & 0xF
        nib[..., 1::2] = words >> 4
        vals = E2M1[nib]
    vals = vals * np.repeat(np.exp2(scales.astype(np.float64) - 127.0), 8, axis=1)[..., None]
    return vals.transpose(0, 1, 3, 2).reshape(g * 512, n)

def pack4(w):
    words, scales = pack_weight(w, "e2m1")
    return words.reshape(words.shape[0], 128, -1), scales


def unpack4(words, scales):
    return unpack_weight(words.reshape(words.shape[0], 128, -1, 2), scales, "e2m1")


B, H = 512, 1024
K = 2 * H
G = 4 * H


def sigmoid(v):
    return 1.0 / (1.0 + np.exp(-v))


def setup_inputs():
    s = mx_kscale(K)
    x = bf(np.random.standard_normal((B, H)) * s[:H])
    h_prev = bf(np.random.standard_normal((B, H)) * s[H:])
    c_prev = bf(np.random.standard_normal((B, H)))
    is_rnn = bf(np.random.random((B, 1)))
    words, scales = pack4(np.random.standard_normal((K, G)) / np.sqrt(K) / s[:, None])
    b = bf(np.random.standard_normal(G) * 0.3)
    return {"x": x,
            "h_prev": h_prev,
            "c_prev": c_prev,
            "is_rnn": is_rnn,
            "W_words": words,
            "W_scales": scales,
            "b": b}


def reference(x, h_prev, c_prev, is_rnn, W_words, W_scales, b):
    c_prev, m = f64(c_prev), f64(is_rnn)
    xh = np.concatenate([f64(x), f64(h_prev)], axis=1)
    gates = (mxq(xh, 1, "e4m3") @ unpack4(W_words, W_scales)) + f64(b)
    i = sigmoid(gates[:, :H])
    f = sigmoid(gates[:, H:2 * H])
    g = np.tanh(gates[:, 2 * H:3 * H])
    o = sigmoid(gates[:, 3 * H:])
    c = f * c_prev + i * g
    c = c * m + c_prev * (1.0 - m)
    o = o * m + (1.0 - m)
    return c, o

@@ -1,0 +1,248 @@
+from contextlib import ExitStack
+
+import concourse.mybir as mybir
+from concourse.masks import make_identity
+
+F32 = mybir.dt.float32
+BF16 = mybir.dt.bfloat16
+I32 = mybir.dt.int32
+U8 = mybir.dt.uint8
+U32 = mybir.dt.uint32
+FP8X4 = mybir.dt.float8_e4m3fn_x4
+FP4X4 = mybir.dt.float4_e2m1fn_x4
+ACT = mybir.ActivationFunctionType
+ALU = mybir.AluOpType
+
+P = 128
+BATCH = 512
+HIDDEN = 1024
+PACK = 4
+K_PASS = P * PACK
+K_GROUPS = 2 * HIDDEN // K_PASS
+SOURCE_GROUPS = HIDDEN // K_PASS
+ROW_TILES = BATCH // P
+N_TILE = 512
+HALVES = HIDDEN // N_TILE
+GATE_I, GATE_F, GATE_G, GATE_O = 0, 1, 2, 3
+GATES = 4
+GATE_ORDER = (GATE_I, GATE_G, GATE_F, GATE_O)
+SCALE_ROWS = K_PASS // 32
+
+FLOPS = 2 * BATCH * 2 * HIDDEN * 4 * HIDDEN
+
+
+def tile_bag_lstm_pa_kernel(tc, x, h_prev, c_prev, is_rnn, W_words, W_scales, b, out_0, out_1):
+    nc = tc.nc
+    with ExitStack() as pools:
+        keep_pool = pools.enter_context(tc.tile_pool(name="keep", bufs=1))
+        stage = pools.enter_context(tc.tile_pool(name="stage", bufs=4))
+        work = pools.enter_context(tc.tile_pool(name="work", bufs=4))
+        psum = pools.enter_context(tc.psum_pool(name="psum", bufs=8))
+        pools.enter_context(tc.manual_schedule())
+
+        ident_f32 = keep_pool.tile([P, P], F32)
+        make_identity(nc, ident_f32[:])
+        ident_bf16 = keep_pool.tile([P, P], BF16)
+        make_identity(nc, ident_bf16[:])
+
+        bias_rows = keep_pool.tile([P, N_TILE], BF16)
+        nc.vector.memset(bias_rows[:], 0.0)
+        nc.scalar.dma_start(
+            out=bias_rows[0 : GATES * HALVES, :], in_=b.rearrange("(c n) -> c n", n=N_TILE)
+        )
+
+        m_rows = keep_pool.tile([P, P], BF16)
+        nc.vector.memset(m_rows[:], 0.0)
+        nc.scalar.dma_start(out=m_rows[0:ROW_TILES, :], in_=is_rnn.rearrange("(t p) o -> t (p o)", p=P))
+
+        warm = keep_pool.tile([P, 1], F32)
+        nc.vector.memset(warm[:], 0.0)
+        nc.scalar.activation(out=warm[:], in_=warm[:], func=ACT.Sigmoid)
+
+        w_words = [
+            keep_pool.tile([P, K_GROUPS, 2 * HIDDEN], U8, align_bytes=64, name="w_words_%d" % gate)
+            for gate in range(GATES)
+        ]
+        w_scales = [
+            keep_pool.tile([P, K_GROUPS, HIDDEN], U8, align_bytes=64, name="w_scales_%d" % gate)
+            for gate in range(GATES)
+        ]
+        for gate in range(GATES):
+            nc.vector.memset(w_scales[gate][:].bitcast(I32), 0)
+
+        def load_gate_weights(gate):
+            scale_rows = W_scales.rearrange("g q n -> q g n")
+            for q in range(SCALE_ROWS // 2):
+                first = 32 * (q // 4) + q % 4
+                nc.sync.dma_start(
+                    out=w_scales[gate][first:P:64, :, :].bitcast(I32),
+                    in_=scale_rows[q : SCALE_ROWS : 8, :, gate * HIDDEN : (gate + 1) * HIDDEN].bitcast(I32),
+                )
+            for group in range(K_GROUPS):
+                nc.sync.dma_start(
+                    out=w_words[gate][:, group, :].bitcast(I32),
+                    in_=W_words[group, :, 2 * gate * HIDDEN : 2 * (gate + 1) * HIDDEN].bitcast(I32),
+                )
+
+        raw = {}
+        for tile_index in range(ROW_TILES):
+            rows = slice(tile_index * P, (tile_index + 1) * P)
+            for source_index, source in enumerate((x, h_prev)):
+                raw_tile = keep_pool.tile([P, HIDDEN], BF16, name="raw_%d_%d" % (tile_index, source_index))
+                nc.sync.dma_start(out=raw_tile[:], in_=source[rows, :])
+                raw[(tile_index, source_index)] = raw_tile
+        load_gate_weights(GATE_I)
+        load_gate_weights(GATE_G)
+        c_old = keep_pool.tile([P, ROW_TILES, HIDDEN], BF16)
+        nc.sync.dma_start(out=c_old[:], in_=c_prev.rearrange("(t p) c -> p t c", p=P))
+        load_gate_weights(GATE_F)
+        load_gate_weights(GATE_O)
+
+        bias_all = keep_pool.tile([P, GATES * HIDDEN], BF16)
+        xq_codes = [
+            keep_pool.tile([P, K_GROUPS, P], U32, align_bytes=64, name="xq_codes_%d" % tile_index)
+            for tile_index in range(ROW_TILES)
+        ]
+        xq_scales = [
+            keep_pool.tile([P, K_GROUPS, P], U8, align_bytes=64, name="xq_scales_%d" % tile_index)
+            for tile_index in range(ROW_TILES)
+        ]
+
+        def spread_bias(gate):
+            spread = psum.tile([P, HIDDEN], BF16, tag="bank")
+            for half in range(HALVES):
+                c = gate * HALVES + half
+                nc.tensor.matmul(
+                    out=spread[:, half * N_TILE : (half + 1) * N_TILE],
+                    lhsT=ident_bf16[:, c : c + 1].to_broadcast([P, P]),
+                    rhs=bias_rows[:],
+                    start=True,
+                    stop=True,
+                )
+            nc.scalar.copy(out=bias_all[:, gate * HIDDEN : (gate + 1) * HIDDEN], in_=spread[:])
+
+        def quantise_rows(tile_index, source_index):
+            words = raw[(tile_index, source_index)][:].bitcast(F32)
+            flipped = psum.tile([P, SOURCE_GROUPS, 2, P], F32, tag="bank")
+            for group in range(SOURCE_GROUPS):
+                for u in range(2):
+                    nc.tensor.transpose(
+                        flipped[:, group, u, :],
+                        words[:, 256 * group + u : 256 * (group + 1) : 2],
+                        ident_f32[:],
+                    )
+            grouped = stage.tile([P, SOURCE_GROUPS, P, PACK], BF16, align_bytes=64)
+            copy_out = nc.vector.tensor_copy if source_index == 0 else nc.scalar.copy
+            copy_out(out=grouped[:].bitcast(F32), in_=flipped[:].rearrange("p g u r -> p g r u"))
+            groups = slice(source_index * SOURCE_GROUPS, (source_index + 1) * SOURCE_GROUPS)
+            nc.vector.quantize_mx(
+                out=xq_codes[tile_index][:, groups, :].rearrange("p g r -> p (g r)").bitcast(FP8X4),
+                scales=xq_scales[tile_index][:, groups, :].rearrange("p g r -> p (g r)"),
+                in_=grouped[:].rearrange("p g r t -> p (g r t)"),
+            )
+
+        for tile_index, gate in enumerate(GATE_ORDER):
+            quantise_rows(tile_index, 0)
+            quantise_rows(tile_index, 1)
+            spread_bias(gate)
+
+        m_flipped = psum.tile([P, P], BF16, tag="bank")
+        nc.tensor.transpose(m_flipped[:], m_rows[:], ident_bf16[:])
+        m_col = keep_pool.tile([P, ROW_TILES], F32)
+        nc.vector.tensor_copy(out=m_col[:], in_=m_flipped[:, 0:ROW_TILES])
+        one_minus_m = keep_pool.tile([P, ROW_TILES], F32)
+        nc.vector.tensor_scalar(
+            out=one_minus_m[:], in0=m_col[:], scalar1=-1.0, scalar2=1.0, op0=ALU.mult, op1=ALU.add
+        )
+
+        in_gate = keep_pool.tile([P, ROW_TILES, HIDDEN], F32)
+        old_part = keep_pool.tile([P, ROW_TILES, HIDDEN], F32)
+        new_part = keep_pool.tile([P, ROW_TILES, HIDDEN], F32)
+
+        def preactivation(gate, tile_index, half):
+            acc = psum.tile([P, N_TILE], F32, tag="bank")
+            for group in range(K_GROUPS):
+                nc.tensor.matmul_mx(
+                    out=acc[:],
+                    lhsT=xq_codes[tile_index][:, group, :].bitcast(FP8X4),
+                    lhsT_scale=xq_scales[tile_index][:, group, :],
+                    rhs=w_words[gate][:, group, 2 * half * N_TILE : 2 * (half + 1) * N_TILE].bitcast(FP4X4),
+                    rhs_scale=w_scales[gate][:, group, half * N_TILE : (half + 1) * N_TILE],
+                    start=(group == 0),
+                    stop=(group == K_GROUPS - 1),
+                )
+            z = work.tile([P, N_TILE], F32)
+            first = gate * HIDDEN + half * N_TILE
+            nc.vector.tensor_tensor(out=z[:], in0=acc[:], in1=bias_all[:, first : first + N_TILE], op=ALU.add)
+            return z
+
+        def unit_views(tile_index, half):
+            rows = slice(tile_index * P, (tile_index + 1) * P)
+            cols = slice(half * N_TILE, (half + 1) * N_TILE)
+            m = m_col[:, tile_index : tile_index + 1]
+            rest = one_minus_m[:, tile_index : tile_index + 1]
+            return rows, cols, m, rest
+
+        def input_gate(tile_index, half):
+            rows, cols, m, rest = unit_views(tile_index, half)
+            z = preactivation(GATE_I, tile_index, half)
+            nc.scalar.activation(out=in_gate[:, tile_index, cols], in_=z[:], func=ACT.Sigmoid)
+
+        def candidate_gate(tile_index, half):
+            z = preactivation(GATE_G, tile_index, half)
+            candidate = work.tile([P, N_TILE], F32)
+            nc.scalar.activation(out=candidate[:], in_=z[:], func=ACT.Tanh)
+            return candidate
+
+        def new_product(tile_index, half, candidate):
+            rows, cols, m, rest = unit_views(tile_index, half)
+            nc.vector.scalar_tensor_tensor(
+                out=new_part[:, tile_index, cols],
+                in0=in_gate[:, tile_index, cols],
+                scalar=m,
+                in1=candidate[:],
+                op0=ALU.mult,
+                op1=ALU.mult,
+            )
+
+        def forget_gate(tile_index, half):
+            rows, cols, m, rest = unit_views(tile_index, half)
+            z = preactivation(GATE_F, tile_index, half)
+            forget = work.tile([P, N_TILE], F32)
+            nc.scalar.activation(out=forget[:], in_=z[:], func=ACT.Sigmoid)
+            retain = work.tile([P, N_TILE], F32)
+            nc.scalar.activation(out=retain[:], in_=forget[:], func=ACT.Identity, scale=m, bias=rest)
+            nc.gpsimd.tensor_tensor(
+                out=old_part[:, tile_index, cols], in0=retain[:], in1=c_old[:, tile_index, cols], op=ALU.mult
+            )
+
+        def output_gate(tile_index, half):
+            rows, cols, m, rest = unit_views(tile_index, half)
+            z = preactivation(GATE_O, tile_index, half)
+            c_new = work.tile([P, N_TILE], F32)
+            nc.vector.tensor_tensor(
+                out=c_new[:], in0=new_part[:, tile_index, cols], in1=old_part[:, tile_index, cols], op=ALU.add
+            )
+            nc.sync.dma_start(out=out_0[rows, cols], in_=c_new[:])
+            out_gate = work.tile([P, N_TILE], F32)
+            nc.scalar.activation(out=out_gate[:], in_=z[:], func=ACT.Sigmoid)
+            o_new = work.tile([P, N_TILE], F32)
+            nc.scalar.activation(out=o_new[:], in_=out_gate[:], func=ACT.Identity, scale=m, bias=rest)
+            nc.sync.dma_start(out=out_1[rows, cols], in_=o_new[:])
+
+        units = [(tile_index, half) for tile_index in range(ROW_TILES) for half in range(HALVES)]
+        for tile_index, half in units:
+            input_gate(tile_index, half)
+        late = None
+        for tile_index, half in units:
+            candidate = candidate_gate(tile_index, half)
+            if late is not None:
+                new_product(*late)
+            late = (tile_index, half, candidate)
+        for tile_index, half in units:
+            forget_gate(tile_index, half)
+            if late is not None:
+                new_product(*late)
+                late = None
+        for tile_index, half in units:
+            output_gate(tile_index, half)

@@ -27,8 +27,9 @@ GATE_I, GATE_F, GATE_G, GATE_O = 0, 1, 2, 3
 GATES = 4
 GATE_ORDER = (GATE_I, GATE_G, GATE_F, GATE_O)
 SCALE_ROWS = K_PASS // 32
+ROUND_TILES = 2
 
-FLOPS = 2 * BATCH * 2 * HIDDEN * 4 * HIDDEN
+FLOPS = 2 * BATCH * 2 * HIDDEN * GATES * HIDDEN
 
 
 def tile_bag_lstm_pa_kernel(tc, x, h_prev, c_prev, is_rnn, W_words, W_scales, b, out_0, out_1):
@@ -40,24 +41,19 @@ def tile_bag_lstm_pa_kernel(tc, x, h_prev, c_prev, is_rnn, W_words, W_scales, b,
         psum = pools.enter_context(tc.psum_pool(name="psum", bufs=8))
         pools.enter_context(tc.manual_schedule())
 
-        ident_f32 = keep_pool.tile([P, P], F32)
-        make_identity(nc, ident_f32[:])
-        ident_bf16 = keep_pool.tile([P, P], BF16)
-        make_identity(nc, ident_bf16[:])
-
         bias_rows = keep_pool.tile([P, N_TILE], BF16)
         nc.vector.memset(bias_rows[:], 0.0)
         nc.scalar.dma_start(
             out=bias_rows[0 : GATES * HALVES, :], in_=b.rearrange("(c n) -> c n", n=N_TILE)
         )
-
         m_rows = keep_pool.tile([P, P], BF16)
         nc.vector.memset(m_rows[:], 0.0)
         nc.scalar.dma_start(out=m_rows[0:ROW_TILES, :], in_=is_rnn.rearrange("(t p) o -> t (p o)", p=P))
 
-        warm = keep_pool.tile([P, 1], F32)
-        nc.vector.memset(warm[:], 0.0)
-        nc.scalar.activation(out=warm[:], in_=warm[:], func=ACT.Sigmoid)
+        ident_bf16 = keep_pool.tile([P, P], BF16)
+        make_identity(nc, ident_bf16[:])
+        ident_f32 = keep_pool.tile([P, P], F32)
+        make_identity(nc, ident_f32[:])
 
         w_words = [
             keep_pool.tile([P, K_GROUPS, 2 * HIDDEN], U8, align_bytes=64, name="w_words_%d" % gate)
@@ -67,38 +63,52 @@ def tile_bag_lstm_pa_kernel(tc, x, h_prev, c_prev, is_rnn, W_words, W_scales, b,
             keep_pool.tile([P, K_GROUPS, HIDDEN], U8, align_bytes=64, name="w_scales_%d" % gate)
             for gate in range(GATES)
         ]
-        for gate in range(GATES):
+        for gate in GATE_ORDER:
             nc.vector.memset(w_scales[gate][:].bitcast(I32), 0)
 
-        def load_gate_weights(gate):
+        warm = keep_pool.tile([P, 1], F32)
+        nc.vector.memset(warm[:], 0.0)
+        nc.scalar.activation(out=warm[:], in_=warm[:], func=ACT.Sigmoid)
+
+        raw = {}
+
+        def load_rows(tile_index):
+            rows = slice(tile_index * P, (tile_index + 1) * P)
+            for source_index, source in enumerate((x, h_prev)):
+                raw_tile = keep_pool.tile([P, HIDDEN], BF16, name="raw_%d_%d" % (tile_index, source_index))
+                nc.sync.dma_start(out=raw_tile[:], in_=source[rows, :])
+                raw[(tile_index, source_index)] = raw_tile
+
+        def load_gate_scales(gate):
             scale_rows = W_scales.rearrange("g q n -> q g n")
-            for q in range(SCALE_ROWS // 2):
-                first = 32 * (q // 4) + q % 4
+            for r in range(4):
                 nc.sync.dma_start(
-                    out=w_scales[gate][first:P:64, :, :].bitcast(I32),
-                    in_=scale_rows[q : SCALE_ROWS : 8, :, gate * HIDDEN : (gate + 1) * HIDDEN].bitcast(I32),
+                    out=w_scales[gate][r:P:32, :, :].bitcast(I32),
+                    in_=scale_rows[r:SCALE_ROWS:4, :, gate * HIDDEN : (gate + 1) * HIDDEN].bitcast(I32),
                 )
+
+        def load_gate_words(gate):
             for group in range(K_GROUPS):
                 nc.sync.dma_start(
                     out=w_words[gate][:, group, :].bitcast(I32),
                     in_=W_words[group, :, 2 * gate * HIDDEN : 2 * (gate + 1) * HIDDEN].bitcast(I32),
                 )
 
-        raw = {}
-        for tile_index in range(ROW_TILES):
-            rows = slice(tile_index * P, (tile_index + 1) * P)
-            for source_index, source in enumerate((x, h_prev)):
-                raw_tile = keep_pool.tile([P, HIDDEN], BF16, name="raw_%d_%d" % (tile_index, source_index))
-                nc.sync.dma_start(out=raw_tile[:], in_=source[rows, :])
-                raw[(tile_index, source_index)] = raw_tile
-        load_gate_weights(GATE_I)
-        load_gate_weights(GATE_G)
+        load_rows(0)
+        load_gate_scales(GATE_I)
+        for tile_index in range(1, ROW_TILES):
+            load_rows(tile_index)
+        load_gate_words(GATE_I)
+        load_gate_scales(GATE_G)
+        load_gate_words(GATE_G)
         c_old = keep_pool.tile([P, ROW_TILES, HIDDEN], BF16)
         nc.sync.dma_start(out=c_old[:], in_=c_prev.rearrange("(t p) c -> p t c", p=P))
-        load_gate_weights(GATE_F)
-        load_gate_weights(GATE_O)
+        load_gate_scales(GATE_F)
+        load_gate_words(GATE_F)
+        load_gate_scales(GATE_O)
+        load_gate_words(GATE_O)
 
-        bias_all = keep_pool.tile([P, GATES * HIDDEN], BF16)
+        bias_all = [keep_pool.tile([P, HIDDEN], BF16, name="bias_all_%d" % gate) for gate in range(GATES)]
         xq_codes = [
             keep_pool.tile([P, K_GROUPS, P], U32, align_bytes=64, name="xq_codes_%d" % tile_index)
             for tile_index in range(ROW_TILES)
@@ -119,7 +129,7 @@ def tile_bag_lstm_pa_kernel(tc, x, h_prev, c_prev, is_rnn, W_words, W_scales, b,
                     start=True,
                     stop=True,
                 )
-            nc.scalar.copy(out=bias_all[:, gate * HIDDEN : (gate + 1) * HIDDEN], in_=spread[:])
+            nc.scalar.copy(out=bias_all[gate][:], in_=spread[:])
 
         def quantise_rows(tile_index, source_index):
             words = raw[(tile_index, source_index)][:].bitcast(F32)
@@ -141,10 +151,12 @@ def tile_bag_lstm_pa_kernel(tc, x, h_prev, c_prev, is_rnn, W_words, W_scales, b,
                 in_=grouped[:].rearrange("p g r t -> p (g r t)"),
             )
 
-        for tile_index, gate in enumerate(GATE_ORDER):
-            quantise_rows(tile_index, 0)
-            quantise_rows(tile_index, 1)
-            spread_bias(gate)
+        for first in range(0, ROW_TILES, ROUND_TILES):
+            for step in range(first, first + ROUND_TILES):
+                spread_bias(GATE_ORDER[step])
+            for tile_index in range(first, first + ROUND_TILES):
+                quantise_rows(tile_index, 0)
+                quantise_rows(tile_index, 1)
 
         m_flipped = psum.tile([P, P], BF16, tag="bank")
         nc.tensor.transpose(m_flipped[:], m_rows[:], ident_bf16[:])
@@ -155,11 +167,17 @@ def tile_bag_lstm_pa_kernel(tc, x, h_prev, c_prev, is_rnn, W_words, W_scales, b,
             out=one_minus_m[:], in0=m_col[:], scalar1=-1.0, scalar2=1.0, op0=ALU.mult, op1=ALU.add
         )
 
-        in_gate = keep_pool.tile([P, ROW_TILES, HIDDEN], F32)
-        old_part = keep_pool.tile([P, ROW_TILES, HIDDEN], F32)
-        new_part = keep_pool.tile([P, ROW_TILES, HIDDEN], F32)
+        units = [(tile_index, half) for tile_index in range(ROW_TILES) for half in range(HALVES)]
+        in_gate = {}
+        new_part = {}
+        old_part = {}
 
-        def preactivation(gate, tile_index, half):
+        def unit_tile(label, unit):
+            return keep_pool.tile([P, N_TILE], F32, name="%s_%d_%d" % (label, unit[0], unit[1]))
+
+        def preactivation(gate, unit):
+            tile_index, half = unit
+            cols = slice(half * N_TILE, (half + 1) * N_TILE)
             acc = psum.tile([P, N_TILE], F32, tag="bank")
             for group in range(K_GROUPS):
                 nc.tensor.matmul_mx(
@@ -167,82 +185,95 @@ def tile_bag_lstm_pa_kernel(tc, x, h_prev, c_prev, is_rnn, W_words, W_scales, b,
                     lhsT=xq_codes[tile_index][:, group, :].bitcast(FP8X4),
                     lhsT_scale=xq_scales[tile_index][:, group, :],
                     rhs=w_words[gate][:, group, 2 * half * N_TILE : 2 * (half + 1) * N_TILE].bitcast(FP4X4),
-                    rhs_scale=w_scales[gate][:, group, half * N_TILE : (half + 1) * N_TILE],
+                    rhs_scale=w_scales[gate][:, group, cols],
                     start=(group == 0),
                     stop=(group == K_GROUPS - 1),
                 )
             z = work.tile([P, N_TILE], F32)
-            first = gate * HIDDEN + half * N_TILE
-            nc.vector.tensor_tensor(out=z[:], in0=acc[:], in1=bias_all[:, first : first + N_TILE], op=ALU.add)
+            nc.vector.tensor_tensor(out=z[:], in0=acc[:], in1=bias_all[gate][:, cols], op=ALU.add)
             return z
 
-        def unit_views(tile_index, half):
-            rows = slice(tile_index * P, (tile_index + 1) * P)
-            cols = slice(half * N_TILE, (half + 1) * N_TILE)
-            m = m_col[:, tile_index : tile_index + 1]
-            rest = one_minus_m[:, tile_index : tile_index + 1]
-            return rows, cols, m, rest
+        def blend(out, gate_values, tile_index):
+            nc.scalar.activation(
+                out=out,
+                in_=gate_values,
+                func=ACT.Identity,
+                scale=m_col[:, tile_index : tile_index + 1],
+                bias=one_minus_m[:, tile_index : tile_index + 1],
+            )
 
-        def input_gate(tile_index, half):
-            rows, cols, m, rest = unit_views(tile_index, half)
-            z = preactivation(GATE_I, tile_index, half)
-            nc.scalar.activation(out=in_gate[:, tile_index, cols], in_=z[:], func=ACT.Sigmoid)
+        def input_gate(unit):
+            z = preactivation(GATE_I, unit)
+            in_gate[unit] = unit_tile("in_gate", unit)
+            nc.scalar.activation(out=in_gate[unit][:], in_=z[:], func=ACT.Sigmoid)
 
-        def candidate_gate(tile_index, half):
-            z = preactivation(GATE_G, tile_index, half)
+        def candidate_gate(unit):
+            z = preactivation(GATE_G, unit)
             candidate = work.tile([P, N_TILE], F32)
             nc.scalar.activation(out=candidate[:], in_=z[:], func=ACT.Tanh)
             return candidate
 
-        def new_product(tile_index, half, candidate):
-            rows, cols, m, rest = unit_views(tile_index, half)
+        def new_product(unit, candidate):
+            tile_index = unit[0]
+            new_part[unit] = unit_tile("new_part", unit)
             nc.vector.scalar_tensor_tensor(
-                out=new_part[:, tile_index, cols],
-                in0=in_gate[:, tile_index, cols],
-                scalar=m,
+                out=new_part[unit][:],
+                in0=in_gate[unit][:],
+                scalar=m_col[:, tile_index : tile_index + 1],
                 in1=candidate[:],
                 op0=ALU.mult,
                 op1=ALU.mult,
             )
 
-        def forget_gate(tile_index, half):
-            rows, cols, m, rest = unit_views(tile_index, half)
-            z = preactivation(GATE_F, tile_index, half)
+        def forget_gate(unit):
+            z = preactivation(GATE_F, unit)
             forget = work.tile([P, N_TILE], F32)
             nc.scalar.activation(out=forget[:], in_=z[:], func=ACT.Sigmoid)
+            return forget
+
+        def old_product(unit, forget):
+            tile_index, half = unit
             retain = work.tile([P, N_TILE], F32)
-            nc.scalar.activation(out=retain[:], in_=forget[:], func=ACT.Identity, scale=m, bias=rest)
+            blend(retain[:], forget[:], tile_index)
+            old_part[unit] = unit_tile("old_part", unit)
             nc.gpsimd.tensor_tensor(
-                out=old_part[:, tile_index, cols], in0=retain[:], in1=c_old[:, tile_index, cols], op=ALU.mult
+                out=old_part[unit][:],
+                in0=retain[:],
+                in1=c_old[:, tile_index, half * N_TILE : (half + 1) * N_TILE],
+                op=ALU.mult,
             )
 
-        def output_gate(tile_index, half):
-            rows, cols, m, rest = unit_views(tile_index, half)
-            z = preactivation(GATE_O, tile_index, half)
+        def output_gate(unit):
+            tile_index, half = unit
+            z = preactivation(GATE_O, unit)
             c_new = work.tile([P, N_TILE], F32)
-            nc.vector.tensor_tensor(
-                out=c_new[:], in0=new_part[:, tile_index, cols], in1=old_part[:, tile_index, cols], op=ALU.add
+            nc.vector.tensor_tensor(out=c_new[:], in0=new_part[unit][:], in1=old_part[unit][:], op=ALU.add)
+            nc.sync.dma_start(
+                out=out_0[tile_index * P : (tile_index + 1) * P, half * N_TILE : (half + 1) * N_TILE], in_=c_new[:]
             )
-            nc.sync.dma_start(out=out_0[rows, cols], in_=c_new[:])
             out_gate = work.tile([P, N_TILE], F32)
             nc.scalar.activation(out=out_gate[:], in_=z[:], func=ACT.Sigmoid)
-            o_new = work.tile([P, N_TILE], F32)
-            nc.scalar.activation(out=o_new[:], in_=out_gate[:], func=ACT.Identity, scale=m, bias=rest)
-            nc.sync.dma_start(out=out_1[rows, cols], in_=o_new[:])
+            return out_gate
 
-        units = [(tile_index, half) for tile_index in range(ROW_TILES) for half in range(HALVES)]
-        for tile_index, half in units:
-            input_gate(tile_index, half)
-        late = None
-        for tile_index, half in units:
-            candidate = candidate_gate(tile_index, half)
-            if late is not None:
-                new_product(*late)
-            late = (tile_index, half, candidate)
-        for tile_index, half in units:
-            forget_gate(tile_index, half)
-            if late is not None:
-                new_product(*late)
-                late = None
-        for tile_index, half in units:
-            output_gate(tile_index, half)
+        def store_output(unit, out_gate):
+            tile_index, half = unit
+            o_new = work.tile([P, N_TILE], F32)
+            blend(o_new[:], out_gate[:], tile_index)
+            nc.sync.dma_start(
+                out=out_1[tile_index * P : (tile_index + 1) * P, half * N_TILE : (half + 1) * N_TILE], in_=o_new[:]
+            )
+
+        for unit in units:
+            input_gate(unit)
+        follow_up, late = None, None
+        for first_part, second_part in (
+            (candidate_gate, new_product),
+            (forget_gate, old_product),
+            (output_gate, store_output),
+        ):
+            for unit in units:
+                activated = first_part(unit)
+                if late is not None:
+                    follow_up(*late)
+                follow_up, late = second_part, (unit, activated)
+        follow_up(*late)

@@ -25,9 +25,9 @@ N_TILE = 512
 HALVES = HIDDEN // N_TILE
 GATE_I, GATE_F, GATE_G, GATE_O = 0, 1, 2, 3
 GATES = 4
-GATE_ORDER = (GATE_I, GATE_G, GATE_F, GATE_O)
+GATE_ORDER = (GATE_F, GATE_I, GATE_G, GATE_O)
 SCALE_ROWS = K_PASS // 32
-ROUND_TILES = 2
+WARM_UP_MATMULS = 3
 
 FLOPS = 2 * BATCH * 2 * HIDDEN * GATES * HIDDEN
 
@@ -36,39 +36,42 @@ def tile_bag_lstm_pa_kernel(tc, x, h_prev, c_prev, is_rnn, W_words, W_scales, b,
     nc = tc.nc
     with ExitStack() as pools:
         keep_pool = pools.enter_context(tc.tile_pool(name="keep", bufs=1))
-        stage = pools.enter_context(tc.tile_pool(name="stage", bufs=4))
+        stage = pools.enter_context(tc.tile_pool(name="stage", bufs=3))
         work = pools.enter_context(tc.tile_pool(name="work", bufs=4))
         psum = pools.enter_context(tc.psum_pool(name="psum", bufs=8))
         pools.enter_context(tc.manual_schedule())
 
         bias_rows = keep_pool.tile([P, N_TILE], BF16)
-        nc.vector.memset(bias_rows[:], 0.0)
-        nc.scalar.dma_start(
+        nc.gpsimd.memset(bias_rows[:].bitcast(F32), 0.0)
+        nc.sync.dma_start(
             out=bias_rows[0 : GATES * HALVES, :], in_=b.rearrange("(c n) -> c n", n=N_TILE)
         )
         m_rows = keep_pool.tile([P, P], BF16)
-        nc.vector.memset(m_rows[:], 0.0)
-        nc.scalar.dma_start(out=m_rows[0:ROW_TILES, :], in_=is_rnn.rearrange("(t p) o -> t (p o)", p=P))
+        nc.gpsimd.memset(m_rows[:].bitcast(F32), 0.0)
+        nc.sync.dma_start(out=m_rows[0:ROW_TILES, :], in_=is_rnn.rearrange("(t p) o -> t (p o)", p=P))
+        warm = keep_pool.tile([P, 1], F32)
+        nc.vector.memset(warm[:], 0.0)
+        nc.scalar.activation(out=warm[:], in_=warm[:], func=ACT.Sigmoid)
+        zeros = keep_pool.tile([P, N_TILE], BF16)
+        nc.vector.memset(zeros[:].bitcast(I32), 0)
 
         ident_bf16 = keep_pool.tile([P, P], BF16)
         make_identity(nc, ident_bf16[:])
         ident_f32 = keep_pool.tile([P, P], F32)
         make_identity(nc, ident_f32[:])
 
-        w_words = [
-            keep_pool.tile([P, K_GROUPS, 2 * HIDDEN], U8, align_bytes=64, name="w_words_%d" % gate)
-            for gate in range(GATES)
-        ]
+        w_words = {}
+        for gate in range(GATES):
+            for half in range(HALVES):
+                w_words[(gate, half)] = keep_pool.tile(
+                    [P, K_GROUPS, 2 * N_TILE], U8, align_bytes=64, name="w_words_%d_%d" % (gate, half)
+                )
         w_scales = [
             keep_pool.tile([P, K_GROUPS, HIDDEN], U8, align_bytes=64, name="w_scales_%d" % gate)
             for gate in range(GATES)
         ]
         for gate in GATE_ORDER:
             nc.vector.memset(w_scales[gate][:].bitcast(I32), 0)
-
-        warm = keep_pool.tile([P, 1], F32)
-        nc.vector.memset(warm[:], 0.0)
-        nc.scalar.activation(out=warm[:], in_=warm[:], func=ACT.Sigmoid)
 
         raw = {}
 
@@ -87,26 +90,37 @@ def tile_bag_lstm_pa_kernel(tc, x, h_prev, c_prev, is_rnn, W_words, W_scales, b,
                     in_=scale_rows[r:SCALE_ROWS:4, :, gate * HIDDEN : (gate + 1) * HIDDEN].bitcast(I32),
                 )
 
-        def load_gate_words(gate):
-            for group in range(K_GROUPS):
-                nc.sync.dma_start(
-                    out=w_words[gate][:, group, :].bitcast(I32),
-                    in_=W_words[group, :, 2 * gate * HIDDEN : 2 * (gate + 1) * HIDDEN].bitcast(I32),
-                )
+        def load_gate_words(gate, half):
+            first = 2 * (gate * HIDDEN + half * N_TILE)
+            nc.sync.dma_start(
+                out=w_words[(gate, half)][:].bitcast(I32),
+                in_=W_words[:, :, first : first + 2 * N_TILE].bitcast(I32).rearrange("g p n -> p g n"),
+            )
 
-        load_rows(0)
-        load_gate_scales(GATE_I)
-        for tile_index in range(1, ROW_TILES):
+        c_old = [keep_pool.tile([P, ROW_TILES, N_TILE], BF16, name="c_old_%d" % half) for half in range(HALVES)]
+
+        def load_c_old(half):
+            nc.sync.dma_start(
+                out=c_old[half][:],
+                in_=c_prev.rearrange("(t p) c -> p t c", p=P)[:, :, half * N_TILE : (half + 1) * N_TILE],
+            )
+
+        for tile_index in range(ROW_TILES):
             load_rows(tile_index)
-        load_gate_words(GATE_I)
-        load_gate_scales(GATE_G)
-        load_gate_words(GATE_G)
-        c_old = keep_pool.tile([P, ROW_TILES, HIDDEN], BF16)
-        nc.sync.dma_start(out=c_old[:], in_=c_prev.rearrange("(t p) c -> p t c", p=P))
         load_gate_scales(GATE_F)
-        load_gate_words(GATE_F)
+        load_gate_words(GATE_F, 0)
+        load_c_old(0)
+        load_gate_scales(GATE_I)
+        load_gate_words(GATE_I, 0)
+        load_gate_scales(GATE_G)
+        load_gate_words(GATE_G, 0)
         load_gate_scales(GATE_O)
-        load_gate_words(GATE_O)
+        load_gate_words(GATE_O, 0)
+        load_gate_words(GATE_F, 1)
+        load_c_old(1)
+        load_gate_words(GATE_I, 1)
+        load_gate_words(GATE_G, 1)
+        load_gate_words(GATE_O, 1)
 
         bias_all = [keep_pool.tile([P, HIDDEN], BF16, name="bias_all_%d" % gate) for gate in range(GATES)]
         xq_codes = [
@@ -131,32 +145,49 @@ def tile_bag_lstm_pa_kernel(tc, x, h_prev, c_prev, is_rnn, W_words, W_scales, b,
                 )
             nc.scalar.copy(out=bias_all[gate][:], in_=spread[:])
 
-        def quantise_rows(tile_index, source_index):
-            words = raw[(tile_index, source_index)][:].bitcast(F32)
-            flipped = psum.tile([P, SOURCE_GROUPS, 2, P], F32, tag="bank")
-            for group in range(SOURCE_GROUPS):
-                for u in range(2):
-                    nc.tensor.transpose(
-                        flipped[:, group, u, :],
-                        words[:, 256 * group + u : 256 * (group + 1) : 2],
-                        ident_f32[:],
-                    )
-            grouped = stage.tile([P, SOURCE_GROUPS, P, PACK], BF16, align_bytes=64)
-            copy_out = nc.vector.tensor_copy if source_index == 0 else nc.scalar.copy
-            copy_out(out=grouped[:].bitcast(F32), in_=flipped[:].rearrange("p g u r -> p g r u"))
-            groups = slice(source_index * SOURCE_GROUPS, (source_index + 1) * SOURCE_GROUPS)
+        grouped = {}
+
+        def flip_rows(tile_index):
+            grouped[tile_index] = stage.tile([P, K_GROUPS, P, PACK], BF16, align_bytes=64, name="grouped")
+            for source_index in range(2):
+                words = raw[(tile_index, source_index)][:].bitcast(F32)
+                flipped = psum.tile([P, SOURCE_GROUPS, 2, P], F32, tag="bank")
+                for group in range(SOURCE_GROUPS):
+                    for u in range(2):
+                        nc.tensor.transpose(
+                            flipped[:, group, u, :],
+                            words[:, 256 * group + u : 256 * (group + 1) : 2],
+                            ident_f32[:],
+                        )
+                groups = slice(source_index * SOURCE_GROUPS, (source_index + 1) * SOURCE_GROUPS)
+                copy_out = nc.vector.tensor_copy if source_index == 0 else nc.scalar.copy
+                copy_out(
+                    out=grouped[tile_index][:, groups, :, :].bitcast(F32),
+                    in_=flipped[:].rearrange("p g u r -> p g r u"),
+                )
+
+        def quantise_rows(tile_index):
             nc.vector.quantize_mx(
-                out=xq_codes[tile_index][:, groups, :].rearrange("p g r -> p (g r)").bitcast(FP8X4),
-                scales=xq_scales[tile_index][:, groups, :].rearrange("p g r -> p (g r)"),
-                in_=grouped[:].rearrange("p g r t -> p (g r t)"),
+                out=xq_codes[tile_index][:].rearrange("p g r -> p (g r)").bitcast(FP8X4),
+                scales=xq_scales[tile_index][:].rearrange("p g r -> p (g r)"),
+                in_=grouped[tile_index][:].rearrange("p g r t -> p (g r t)"),
             )
 
-        for first in range(0, ROW_TILES, ROUND_TILES):
-            for step in range(first, first + ROUND_TILES):
-                spread_bias(GATE_ORDER[step])
-            for tile_index in range(first, first + ROUND_TILES):
-                quantise_rows(tile_index, 0)
-                quantise_rows(tile_index, 1)
+        warm_bank = psum.tile([P, N_TILE], F32, tag="bank")
+        for step in range(WARM_UP_MATMULS):
+            nc.tensor.matmul(out=warm_bank[:], lhsT=zeros[:, 0:P], rhs=zeros[:], start=True, stop=True)
+        spread_bias(GATE_F)
+        spread_bias(GATE_I)
+        flip_rows(0)
+        flip_rows(1)
+        quantise_rows(0)
+        spread_bias(GATE_G)
+        spread_bias(GATE_O)
+        flip_rows(2)
+        quantise_rows(1)
+        flip_rows(3)
+        quantise_rows(2)
+        quantise_rows(3)
 
         m_flipped = psum.tile([P, P], BF16, tag="bank")
         nc.tensor.transpose(m_flipped[:], m_rows[:], ident_bf16[:])
@@ -167,16 +198,23 @@ def tile_bag_lstm_pa_kernel(tc, x, h_prev, c_prev, is_rnn, W_words, W_scales, b,
             out=one_minus_m[:], in0=m_col[:], scalar1=-1.0, scalar2=1.0, op0=ALU.mult, op1=ALU.add
         )
 
-        units = [(tile_index, half) for tile_index in range(ROW_TILES) for half in range(HALVES)]
         in_gate = {}
         new_part = {}
         old_part = {}
+        later = {}
 
-        def unit_tile(label, unit):
-            return keep_pool.tile([P, N_TILE], F32, name="%s_%d_%d" % (label, unit[0], unit[1]))
+        def write_later(slot, action):
+            later.setdefault(slot, []).append(action)
 
-        def preactivation(gate, unit):
-            tile_index, half = unit
+        def cell_tile(label, cell):
+            return keep_pool.tile([P, N_TILE], F32, name="%s_%d_%d" % (label, cell[0], cell[1]))
+
+        def out_view(out, cell):
+            tile_index, half = cell
+            return out[tile_index * P : (tile_index + 1) * P, half * N_TILE : (half + 1) * N_TILE]
+
+        def preactivation(gate, cell):
+            tile_index, half = cell
             cols = slice(half * N_TILE, (half + 1) * N_TILE)
             acc = psum.tile([P, N_TILE], F32, tag="bank")
             for group in range(K_GROUPS):
@@ -184,7 +222,7 @@ def tile_bag_lstm_pa_kernel(tc, x, h_prev, c_prev, is_rnn, W_words, W_scales, b,
                     out=acc[:],
                     lhsT=xq_codes[tile_index][:, group, :].bitcast(FP8X4),
                     lhsT_scale=xq_scales[tile_index][:, group, :],
-                    rhs=w_words[gate][:, group, 2 * half * N_TILE : 2 * (half + 1) * N_TILE].bitcast(FP4X4),
+                    rhs=w_words[(gate, half)][:, group, :].bitcast(FP4X4),
                     rhs_scale=w_scales[gate][:, group, cols],
                     start=(group == 0),
                     stop=(group == K_GROUPS - 1),
@@ -202,78 +240,76 @@ def tile_bag_lstm_pa_kernel(tc, x, h_prev, c_prev, is_rnn, W_words, W_scales, b,
                 bias=one_minus_m[:, tile_index : tile_index + 1],
             )
 
-        def input_gate(unit):
-            z = preactivation(GATE_I, unit)
-            in_gate[unit] = unit_tile("in_gate", unit)
-            nc.scalar.activation(out=in_gate[unit][:], in_=z[:], func=ACT.Sigmoid)
+        def old_product(cell, forget):
+            tile_index, half = cell
+            retain = work.tile([P, N_TILE], F32)
+            blend(retain[:], forget[:], tile_index)
+            old_part[cell] = cell_tile("old_part", cell)
+            nc.gpsimd.tensor_tensor(
+                out=old_part[cell][:], in0=retain[:], in1=c_old[half][:, tile_index, :], op=ALU.mult
+            )
 
-        def candidate_gate(unit):
-            z = preactivation(GATE_G, unit)
-            candidate = work.tile([P, N_TILE], F32)
-            nc.scalar.activation(out=candidate[:], in_=z[:], func=ACT.Tanh)
-            return candidate
-
-        def new_product(unit, candidate):
-            tile_index = unit[0]
-            new_part[unit] = unit_tile("new_part", unit)
+        def new_product(cell, candidate):
+            tile_index = cell[0]
+            new_part[cell] = cell_tile("new_part", cell)
             nc.vector.scalar_tensor_tensor(
-                out=new_part[unit][:],
-                in0=in_gate[unit][:],
+                out=new_part[cell][:],
+                in0=in_gate[cell][:],
                 scalar=m_col[:, tile_index : tile_index + 1],
                 in1=candidate[:],
                 op0=ALU.mult,
                 op1=ALU.mult,
             )
 
-        def forget_gate(unit):
-            z = preactivation(GATE_F, unit)
-            forget = work.tile([P, N_TILE], F32)
-            nc.scalar.activation(out=forget[:], in_=z[:], func=ACT.Sigmoid)
-            return forget
-
-        def old_product(unit, forget):
-            tile_index, half = unit
-            retain = work.tile([P, N_TILE], F32)
-            blend(retain[:], forget[:], tile_index)
-            old_part[unit] = unit_tile("old_part", unit)
-            nc.gpsimd.tensor_tensor(
-                out=old_part[unit][:],
-                in0=retain[:],
-                in1=c_old[:, tile_index, half * N_TILE : (half + 1) * N_TILE],
-                op=ALU.mult,
-            )
-
-        def output_gate(unit):
-            tile_index, half = unit
-            z = preactivation(GATE_O, unit)
+        def store_cell_state(cell):
             c_new = work.tile([P, N_TILE], F32)
-            nc.vector.tensor_tensor(out=c_new[:], in0=new_part[unit][:], in1=old_part[unit][:], op=ALU.add)
-            nc.sync.dma_start(
-                out=out_0[tile_index * P : (tile_index + 1) * P, half * N_TILE : (half + 1) * N_TILE], in_=c_new[:]
-            )
-            out_gate = work.tile([P, N_TILE], F32)
-            nc.scalar.activation(out=out_gate[:], in_=z[:], func=ACT.Sigmoid)
-            return out_gate
+            nc.vector.tensor_tensor(out=c_new[:], in0=new_part[cell][:], in1=old_part[cell][:], op=ALU.add)
+            nc.sync.dma_start(out=out_view(out_0, cell), in_=c_new[:])
 
-        def store_output(unit, out_gate):
-            tile_index, half = unit
+        def store_output(cell, out_gate):
+            tile_index = cell[0]
             o_new = work.tile([P, N_TILE], F32)
-            blend(o_new[:], out_gate[:], tile_index)
-            nc.sync.dma_start(
-                out=out_1[tile_index * P : (tile_index + 1) * P, half * N_TILE : (half + 1) * N_TILE], in_=o_new[:]
+            nc.vector.tensor_scalar(
+                out=o_new[:],
+                in0=out_gate[:],
+                scalar1=m_col[:, tile_index : tile_index + 1],
+                scalar2=one_minus_m[:, tile_index : tile_index + 1],
+                op0=ALU.mult,
+                op1=ALU.add,
             )
+            nc.sync.dma_start(out=out_view(out_1, cell), in_=o_new[:])
 
-        for unit in units:
-            input_gate(unit)
-        follow_up, late = None, None
-        for first_part, second_part in (
-            (candidate_gate, new_product),
-            (forget_gate, old_product),
-            (output_gate, store_output),
-        ):
-            for unit in units:
-                activated = first_part(unit)
-                if late is not None:
-                    follow_up(*late)
-                follow_up, late = second_part, (unit, activated)
-        follow_up(*late)
+        def unit(slot, gate, cell):
+            z = preactivation(gate, cell)
+            if gate == GATE_I:
+                in_gate[cell] = cell_tile("in_gate", cell)
+                nc.scalar.activation(out=in_gate[cell][:], in_=z[:], func=ACT.Sigmoid)
+            elif gate == GATE_F:
+                forget = work.tile([P, N_TILE], F32)
+                nc.scalar.activation(out=forget[:], in_=z[:], func=ACT.Sigmoid)
+                write_later(slot + 1, lambda: old_product(cell, forget))
+            elif gate == GATE_G:
+                candidate = work.tile([P, N_TILE], F32)
+                nc.scalar.activation(out=candidate[:], in_=z[:], func=ACT.Tanh)
+                write_later(slot + 2, lambda: new_product(cell, candidate))
+                write_later(slot + 3, lambda: store_cell_state(cell))
+            else:
+                out_gate = work.tile([P, N_TILE], F32)
+                nc.scalar.activation(out=out_gate[:], in_=z[:], func=ACT.Sigmoid)
+                write_later(slot + 1, lambda: store_output(cell, out_gate))
+
+        order = []
+        for half in range(HALVES):
+            order.extend([(GATE_F, (tile_index, half)) for tile_index in range(ROW_TILES)])
+            for tile_index in range(ROW_TILES):
+                order.append((GATE_I, (tile_index, half)))
+                order.append((GATE_G, (tile_index, half)))
+            order.extend([(GATE_O, (tile_index, half)) for tile_index in range(ROW_TILES)])
+
+        for slot, (gate, cell) in enumerate(order):
+            unit(slot, gate, cell)
+            for action in later.get(slot, []):
+                action()
+        for slot in range(len(order), len(order) + ROW_TILES + 1):
+            for action in later.get(slot, []):
+                action()

@@ -28,6 +28,8 @@ GATES = 4
 GATE_ORDER = (GATE_F, GATE_I, GATE_G, GATE_O)
 SCALE_ROWS = K_PASS // 32
 WARM_UP_MATMULS = 3
+NARROW = 128
+NARROW_UNITS = 1
 
 FLOPS = 2 * BATCH * 2 * HIDDEN * GATES * HIDDEN
 
@@ -38,6 +40,7 @@ def tile_bag_lstm_pa_kernel(tc, x, h_prev, c_prev, is_rnn, W_words, W_scales, b,
         keep_pool = pools.enter_context(tc.tile_pool(name="keep", bufs=1))
         stage = pools.enter_context(tc.tile_pool(name="stage", bufs=3))
         work = pools.enter_context(tc.tile_pool(name="work", bufs=4))
+        pieces = pools.enter_context(tc.tile_pool(name="pieces", bufs=NARROW_UNITS * N_TILE // NARROW))
         psum = pools.enter_context(tc.psum_pool(name="psum", bufs=8))
         pools.enter_context(tc.manual_schedule())
 
@@ -110,16 +113,16 @@ def tile_bag_lstm_pa_kernel(tc, x, h_prev, c_prev, is_rnn, W_words, W_scales, b,
         load_gate_scales(GATE_F)
         load_gate_words(GATE_F, 0)
         load_c_old(0)
+        load_gate_words(GATE_F, 1)
+        load_c_old(1)
         load_gate_scales(GATE_I)
         load_gate_words(GATE_I, 0)
         load_gate_scales(GATE_G)
         load_gate_words(GATE_G, 0)
-        load_gate_scales(GATE_O)
-        load_gate_words(GATE_O, 0)
-        load_gate_words(GATE_F, 1)
-        load_c_old(1)
         load_gate_words(GATE_I, 1)
         load_gate_words(GATE_G, 1)
+        load_gate_scales(GATE_O)
+        load_gate_words(GATE_O, 0)
         load_gate_words(GATE_O, 1)
 
         bias_all = [keep_pool.tile([P, HIDDEN], BF16, name="bias_all_%d" % gate) for gate in range(GATES)]
@@ -209,25 +212,28 @@ def tile_bag_lstm_pa_kernel(tc, x, h_prev, c_prev, is_rnn, W_words, W_scales, b,
         def cell_tile(label, cell):
             return keep_pool.tile([P, N_TILE], F32, name="%s_%d_%d" % (label, cell[0], cell[1]))
 
-        def out_view(out, cell):
+        def out_view(out, cell, first=0, width=N_TILE):
             tile_index, half = cell
-            return out[tile_index * P : (tile_index + 1) * P, half * N_TILE : (half + 1) * N_TILE]
+            return out[tile_index * P : (tile_index + 1) * P, half * N_TILE + first : half * N_TILE + first + width]
 
-        def preactivation(gate, cell):
+        def pool_of(width):
+            return work if width == N_TILE else pieces
+
+        def preactivation(gate, cell, first, width):
             tile_index, half = cell
-            cols = slice(half * N_TILE, (half + 1) * N_TILE)
-            acc = psum.tile([P, N_TILE], F32, tag="bank")
+            cols = slice(half * N_TILE + first, half * N_TILE + first + width)
+            acc = psum.tile([P, width], F32, tag="bank")
             for group in range(K_GROUPS):
                 nc.tensor.matmul_mx(
                     out=acc[:],
                     lhsT=xq_codes[tile_index][:, group, :].bitcast(FP8X4),
                     lhsT_scale=xq_scales[tile_index][:, group, :],
-                    rhs=w_words[(gate, half)][:, group, :].bitcast(FP4X4),
+                    rhs=w_words[(gate, half)][:, group, 2 * first : 2 * (first + width)].bitcast(FP4X4),
                     rhs_scale=w_scales[gate][:, group, cols],
                     start=(group == 0),
                     stop=(group == K_GROUPS - 1),
                 )
-            z = work.tile([P, N_TILE], F32)
+            z = pool_of(width).tile([P, width], F32, name="z")
             nc.vector.tensor_tensor(out=z[:], in0=acc[:], in1=bias_all[gate][:, cols], op=ALU.add)
             return z
 
@@ -266,9 +272,9 @@ def tile_bag_lstm_pa_kernel(tc, x, h_prev, c_prev, is_rnn, W_words, W_scales, b,
             nc.vector.tensor_tensor(out=c_new[:], in0=new_part[cell][:], in1=old_part[cell][:], op=ALU.add)
             nc.sync.dma_start(out=out_view(out_0, cell), in_=c_new[:])
 
-        def store_output(cell, out_gate):
+        def store_output(cell, first, width, out_gate):
             tile_index = cell[0]
-            o_new = work.tile([P, N_TILE], F32)
+            o_new = pool_of(width).tile([P, width], F32, name="o_new")
             nc.vector.tensor_scalar(
                 out=o_new[:],
                 in0=out_gate[:],
@@ -277,10 +283,10 @@ def tile_bag_lstm_pa_kernel(tc, x, h_prev, c_prev, is_rnn, W_words, W_scales, b,
                 op0=ALU.mult,
                 op1=ALU.add,
             )
-            nc.sync.dma_start(out=out_view(out_1, cell), in_=o_new[:])
+            nc.sync.dma_start(out=out_view(out_1, cell, first, width), in_=o_new[:])
 
-        def unit(slot, gate, cell):
-            z = preactivation(gate, cell)
+        def unit(slot, gate, cell, first, width):
+            z = preactivation(gate, cell, first, width)
             if gate == GATE_I:
                 in_gate[cell] = cell_tile("in_gate", cell)
                 nc.scalar.activation(out=in_gate[cell][:], in_=z[:], func=ACT.Sigmoid)
@@ -294,22 +300,24 @@ def tile_bag_lstm_pa_kernel(tc, x, h_prev, c_prev, is_rnn, W_words, W_scales, b,
                 write_later(slot + 2, lambda: new_product(cell, candidate))
                 write_later(slot + 3, lambda: store_cell_state(cell))
             else:
-                out_gate = work.tile([P, N_TILE], F32)
+                out_gate = pool_of(width).tile([P, width], F32, name="out_gate")
                 nc.scalar.activation(out=out_gate[:], in_=z[:], func=ACT.Sigmoid)
-                write_later(slot + 1, lambda: store_output(cell, out_gate))
+                write_later(slot + 2 * N_TILE // width, lambda: store_output(cell, first, width, out_gate))
 
         order = []
-        for half in range(HALVES):
-            order.extend([(GATE_F, (tile_index, half)) for tile_index in range(ROW_TILES)])
-            for tile_index in range(ROW_TILES):
-                order.append((GATE_I, (tile_index, half)))
-                order.append((GATE_G, (tile_index, half)))
-            order.extend([(GATE_O, (tile_index, half)) for tile_index in range(ROW_TILES)])
+        cells = [(tile_index, half) for half in range(HALVES) for tile_index in range(ROW_TILES)]
+        order.extend([(GATE_F, cell, 0, N_TILE) for cell in cells])
+        for cell in cells:
+            order.append((GATE_I, cell, 0, N_TILE))
+            order.append((GATE_G, cell, 0, N_TILE))
+        order.extend([(GATE_O, cell, 0, N_TILE) for cell in cells[0 : len(cells) - NARROW_UNITS]])
+        for cell in cells[len(cells) - NARROW_UNITS :]:
+            order.extend([(GATE_O, cell, first, NARROW) for first in range(0, N_TILE, NARROW)])
 
-        for slot, (gate, cell) in enumerate(order):
-            unit(slot, gate, cell)
+        for slot, (gate, cell, first, width) in enumerate(order):
+            unit(slot, gate, cell, first, width)
             for action in later.get(slot, []):
                 action()
-        for slot in range(len(order), len(order) + ROW_TILES + 1):
+        for slot in range(len(order), len(order) + 2 * N_TILE // NARROW + 1):
             for action in later.get(slot, []):
                 action()

@@ -67,10 +67,10 @@ def tile_bag_lstm_pa_kernel(tc, x, h_prev, c_prev, is_rnn, W_words, W_scales, b,
         for gate in range(GATES):
             for half in range(HALVES):
                 w_words[(gate, half)] = keep_pool.tile(
-                    [P, K_GROUPS, 2 * N_TILE], U8, align_bytes=64, name="w_words_%d_%d" % (gate, half)
+                    [P, K_GROUPS, 2 * N_TILE], U8, align_bytes=256, name="w_words_%d_%d" % (gate, half)
                 )
         w_scales = [
-            keep_pool.tile([P, K_GROUPS, HIDDEN], U8, align_bytes=64, name="w_scales_%d" % gate)
+            keep_pool.tile([P, K_GROUPS, HIDDEN], U8, align_bytes=256, name="w_scales_%d" % gate)
             for gate in range(GATES)
         ]
         for gate in GATE_ORDER:
@@ -127,11 +127,11 @@ def tile_bag_lstm_pa_kernel(tc, x, h_prev, c_prev, is_rnn, W_words, W_scales, b,
 
         bias_all = [keep_pool.tile([P, HIDDEN], BF16, name="bias_all_%d" % gate) for gate in range(GATES)]
         xq_codes = [
-            keep_pool.tile([P, K_GROUPS, P], U32, align_bytes=64, name="xq_codes_%d" % tile_index)
+            keep_pool.tile([P, K_GROUPS, P], U32, align_bytes=256, name="xq_codes_%d" % tile_index)
             for tile_index in range(ROW_TILES)
         ]
         xq_scales = [
-            keep_pool.tile([P, K_GROUPS, P], U8, align_bytes=64, name="xq_scales_%d" % tile_index)
+            keep_pool.tile([P, K_GROUPS, P], U8, align_bytes=256, name="xq_scales_%d" % tile_index)
             for tile_index in range(ROW_TILES)
         ]
 
@@ -151,7 +151,7 @@ def tile_bag_lstm_pa_kernel(tc, x, h_prev, c_prev, is_rnn, W_words, W_scales, b,
         grouped = {}
 
         def flip_rows(tile_index):
-            grouped[tile_index] = stage.tile([P, K_GROUPS, P, PACK], BF16, align_bytes=64, name="grouped")
+            grouped[tile_index] = stage.tile([P, K_GROUPS, P, PACK], BF16, align_bytes=256, name="grouped")
             for source_index in range(2):
                 words = raw[(tile_index, source_index)][:].bitcast(F32)
                 flipped = psum.tile([P, SOURCE_GROUPS, 2, P], F32, tag="bank")

@@ -28,6 +28,7 @@ GATES = 4
 GATE_ORDER = (GATE_F, GATE_I, GATE_G, GATE_O)
 SCALE_ROWS = K_PASS // 32
 WARM_UP_MATMULS = 3
+ALIGN = 256
 NARROW = 128
 NARROW_UNITS = 1
 
@@ -44,33 +45,33 @@ def tile_bag_lstm_pa_kernel(tc, x, h_prev, c_prev, is_rnn, W_words, W_scales, b,
         psum = pools.enter_context(tc.psum_pool(name="psum", bufs=8))
         pools.enter_context(tc.manual_schedule())
 
-        bias_rows = keep_pool.tile([P, N_TILE], BF16)
+        bias_rows = keep_pool.tile([P, N_TILE], BF16, align_bytes=ALIGN)
         nc.gpsimd.memset(bias_rows[:].bitcast(F32), 0.0)
         nc.sync.dma_start(
             out=bias_rows[0 : GATES * HALVES, :], in_=b.rearrange("(c n) -> c n", n=N_TILE)
         )
-        m_rows = keep_pool.tile([P, P], BF16)
+        m_rows = keep_pool.tile([P, P], BF16, align_bytes=ALIGN)
         nc.gpsimd.memset(m_rows[:].bitcast(F32), 0.0)
         nc.sync.dma_start(out=m_rows[0:ROW_TILES, :], in_=is_rnn.rearrange("(t p) o -> t (p o)", p=P))
-        warm = keep_pool.tile([P, 1], F32)
+        warm = keep_pool.tile([P, 1], F32, align_bytes=ALIGN)
         nc.vector.memset(warm[:], 0.0)
         nc.scalar.activation(out=warm[:], in_=warm[:], func=ACT.Sigmoid)
-        zeros = keep_pool.tile([P, N_TILE], BF16)
+        zeros = keep_pool.tile([P, N_TILE], BF16, align_bytes=ALIGN)
         nc.vector.memset(zeros[:].bitcast(I32), 0)
 
-        ident_bf16 = keep_pool.tile([P, P], BF16)
+        ident_bf16 = keep_pool.tile([P, P], BF16, align_bytes=ALIGN)
         make_identity(nc, ident_bf16[:])
-        ident_f32 = keep_pool.tile([P, P], F32)
+        ident_f32 = keep_pool.tile([P, P], F32, align_bytes=ALIGN)
         make_identity(nc, ident_f32[:])
 
         w_words = {}
         for gate in range(GATES):
             for half in range(HALVES):
                 w_words[(gate, half)] = keep_pool.tile(
-                    [P, K_GROUPS, 2 * N_TILE], U8, align_bytes=256, name="w_words_%d_%d" % (gate, half)
+                    [P, K_GROUPS, 2 * N_TILE], U8, align_bytes=ALIGN, name="w_words_%d_%d" % (gate, half)
                 )
         w_scales = [
-            keep_pool.tile([P, K_GROUPS, HIDDEN], U8, align_bytes=256, name="w_scales_%d" % gate)
+            keep_pool.tile([P, K_GROUPS, HIDDEN], U8, align_bytes=ALIGN, name="w_scales_%d" % gate)
             for gate in range(GATES)
         ]
         for gate in GATE_ORDER:
@@ -81,7 +82,9 @@ def tile_bag_lstm_pa_kernel(tc, x, h_prev, c_prev, is_rnn, W_words, W_scales, b,
         def load_rows(tile_index):
             rows = slice(tile_index * P, (tile_index + 1) * P)
             for source_index, source in enumerate((x, h_prev)):
-                raw_tile = keep_pool.tile([P, HIDDEN], BF16, name="raw_%d_%d" % (tile_index, source_index))
+                raw_tile = keep_pool.tile(
+                    [P, HIDDEN], BF16, align_bytes=ALIGN, name="raw_%d_%d" % (tile_index, source_index)
+                )
                 nc.sync.dma_start(out=raw_tile[:], in_=source[rows, :])
                 raw[(tile_index, source_index)] = raw_tile
 
@@ -100,7 +103,10 @@ def tile_bag_lstm_pa_kernel(tc, x, h_prev, c_prev, is_rnn, W_words, W_scales, b,
                 in_=W_words[:, :, first : first + 2 * N_TILE].bitcast(I32).rearrange("g p n -> p g n"),
             )
 
-        c_old = [keep_pool.tile([P, ROW_TILES, N_TILE], BF16, name="c_old_%d" % half) for half in range(HALVES)]
+        c_old = [
+            keep_pool.tile([P, ROW_TILES, N_TILE], BF16, align_bytes=ALIGN, name="c_old_%d" % half)
+            for half in range(HALVES)
+        ]
 
         def load_c_old(half):
             nc.sync.dma_start(
@@ -125,13 +131,15 @@ def tile_bag_lstm_pa_kernel(tc, x, h_prev, c_prev, is_rnn, W_words, W_scales, b,
         load_gate_words(GATE_O, 0)
         load_gate_words(GATE_O, 1)
 
-        bias_all = [keep_pool.tile([P, HIDDEN], BF16, name="bias_all_%d" % gate) for gate in range(GATES)]
+        bias_all = [
+            keep_pool.tile([P, HIDDEN], BF16, align_bytes=ALIGN, name="bias_all_%d" % gate) for gate in range(GATES)
+        ]
         xq_codes = [
-            keep_pool.tile([P, K_GROUPS, P], U32, align_bytes=256, name="xq_codes_%d" % tile_index)
+            keep_pool.tile([P, K_GROUPS, P], U32, align_bytes=ALIGN, name="xq_codes_%d" % tile_index)
             for tile_index in range(ROW_TILES)
         ]
         xq_scales = [
-            keep_pool.tile([P, K_GROUPS, P], U8, align_bytes=256, name="xq_scales_%d" % tile_index)
+            keep_pool.tile([P, K_GROUPS, P], U8, align_bytes=ALIGN, name="xq_scales_%d" % tile_index)
             for tile_index in range(ROW_TILES)
         ]
 
@@ -151,7 +159,7 @@ def tile_bag_lstm_pa_kernel(tc, x, h_prev, c_prev, is_rnn, W_words, W_scales, b,
         grouped = {}
 
         def flip_rows(tile_index):
-            grouped[tile_index] = stage.tile([P, K_GROUPS, P, PACK], BF16, align_bytes=256, name="grouped")
+            grouped[tile_index] = stage.tile([P, K_GROUPS, P, PACK], BF16, align_bytes=ALIGN, name="grouped")
             for source_index in range(2):
                 words = raw[(tile_index, source_index)][:].bitcast(F32)
                 flipped = psum.tile([P, SOURCE_GROUPS, 2, P], F32, tag="bank")
@@ -194,9 +202,9 @@ def tile_bag_lstm_pa_kernel(tc, x, h_prev, c_prev, is_rnn, W_words, W_scales, b,
 
         m_flipped = psum.tile([P, P], BF16, tag="bank")
         nc.tensor.transpose(m_flipped[:], m_rows[:], ident_bf16[:])
-        m_col = keep_pool.tile([P, ROW_TILES], F32)
+        m_col = keep_pool.tile([P, ROW_TILES], F32, align_bytes=ALIGN)
         nc.vector.tensor_copy(out=m_col[:], in_=m_flipped[:, 0:ROW_TILES])
-        one_minus_m = keep_pool.tile([P, ROW_TILES], F32)
+        one_minus_m = keep_pool.tile([P, ROW_TILES], F32, align_bytes=ALIGN)
         nc.vector.tensor_scalar(
             out=one_minus_m[:], in0=m_col[:], scalar1=-1.0, scalar2=1.0, op0=ALU.mult, op1=ALU.add
         )
@@ -210,7 +218,7 @@ def tile_bag_lstm_pa_kernel(tc, x, h_prev, c_prev, is_rnn, W_words, W_scales, b,
             later.setdefault(slot, []).append(action)
 
         def cell_tile(label, cell):
-            return keep_pool.tile([P, N_TILE], F32, name="%s_%d_%d" % (label, cell[0], cell[1]))
+            return keep_pool.tile([P, N_TILE], F32, align_bytes=ALIGN, name="%s_%d_%d" % (label, cell[0], cell[1]))
 
         def out_view(out, cell, first=0, width=N_TILE):
             tile_index, half = cell
@@ -233,7 +241,7 @@ def tile_bag_lstm_pa_kernel(tc, x, h_prev, c_prev, is_rnn, W_words, W_scales, b,
                     start=(group == 0),
                     stop=(group == K_GROUPS - 1),
                 )
-            z = pool_of(width).tile([P, width], F32, name="z")
+            z = pool_of(width).tile([P, width], F32, align_bytes=ALIGN, name="z")
             nc.vector.tensor_tensor(out=z[:], in0=acc[:], in1=bias_all[gate][:, cols], op=ALU.add)
             return z
 
@@ -248,7 +256,7 @@ def tile_bag_lstm_pa_kernel(tc, x, h_prev, c_prev, is_rnn, W_words, W_scales, b,
 
         def old_product(cell, forget):
             tile_index, half = cell
-            retain = work.tile([P, N_TILE], F32)
+            retain = work.tile([P, N_TILE], F32, align_bytes=ALIGN)
             blend(retain[:], forget[:], tile_index)
             old_part[cell] = cell_tile("old_part", cell)
             nc.gpsimd.tensor_tensor(
@@ -268,13 +276,13 @@ def tile_bag_lstm_pa_kernel(tc, x, h_prev, c_prev, is_rnn, W_words, W_scales, b,
             )
 
         def store_cell_state(cell):
-            c_new = work.tile([P, N_TILE], F32)
+            c_new = work.tile([P, N_TILE], F32, align_bytes=ALIGN)
             nc.vector.tensor_tensor(out=c_new[:], in0=new_part[cell][:], in1=old_part[cell][:], op=ALU.add)
             nc.sync.dma_start(out=out_view(out_0, cell), in_=c_new[:])
 
         def store_output(cell, first, width, out_gate):
             tile_index = cell[0]
-            o_new = pool_of(width).tile([P, width], F32, name="o_new")
+            o_new = pool_of(width).tile([P, width], F32, align_bytes=ALIGN, name="o_new")
             nc.vector.tensor_scalar(
                 out=o_new[:],
                 in0=out_gate[:],
@@ -291,16 +299,16 @@ def tile_bag_lstm_pa_kernel(tc, x, h_prev, c_prev, is_rnn, W_words, W_scales, b,
                 in_gate[cell] = cell_tile("in_gate", cell)
                 nc.scalar.activation(out=in_gate[cell][:], in_=z[:], func=ACT.Sigmoid)
             elif gate == GATE_F:
-                forget = work.tile([P, N_TILE], F32)
+                forget = work.tile([P, N_TILE], F32, align_bytes=ALIGN)
                 nc.scalar.activation(out=forget[:], in_=z[:], func=ACT.Sigmoid)
                 write_later(slot + 1, lambda: old_product(cell, forget))
             elif gate == GATE_G:
-                candidate = work.tile([P, N_TILE], F32)
+                candidate = work.tile([P, N_TILE], F32, align_bytes=ALIGN)
                 nc.scalar.activation(out=candidate[:], in_=z[:], func=ACT.Tanh)
                 write_later(slot + 2, lambda: new_product(cell, candidate))
                 write_later(slot + 3, lambda: store_cell_state(cell))
             else:
-                out_gate = pool_of(width).tile([P, width], F32, name="out_gate")
+                out_gate = pool_of(width).tile([P, width], F32, align_bytes=ALIGN, name="out_gate")
                 nc.scalar.activation(out=out_gate[:], in_=z[:], func=ACT.Sigmoid)
                 write_later(slot + 2 * N_TILE // width, lambda: store_output(cell, first, width, out_gate))
 
@@ -314,10 +322,16 @@ def tile_bag_lstm_pa_kernel(tc, x, h_prev, c_prev, is_rnn, W_words, W_scales, b,
         for cell in cells[len(cells) - NARROW_UNITS :]:
             order.extend([(GATE_O, cell, first, NARROW) for first in range(0, N_TILE, NARROW)])
 
+        postponed = []
         for slot, (gate, cell, first, width) in enumerate(order):
             unit(slot, gate, cell, first, width)
-            for action in later.get(slot, []):
-                action()
+            if width == N_TILE:
+                for action in later.get(slot, []):
+                    action()
+            else:
+                postponed.extend(later.get(slot, []))
+        for action in postponed:
+            action()
         for slot in range(len(order), len(order) + 2 * N_TILE // NARROW + 1):
             for action in later.get(slot, []):
                 action()

@@ -114,6 +114,9 @@ def tile_bag_lstm_pa_kernel(tc, x, h_prev, c_prev, is_rnn, W_words, W_scales, b,
                 in_=c_prev.rearrange("(t p) c -> p t c", p=P)[:, :, half * N_TILE : (half + 1) * N_TILE],
             )
 
+        bias_all = [
+            keep_pool.tile([P, HIDDEN], BF16, align_bytes=ALIGN, name="bias_all_%d" % gate) for gate in range(GATES)
+        ]
         for tile_index in range(ROW_TILES):
             load_rows(tile_index)
         load_gate_scales(GATE_F)
@@ -130,10 +133,10 @@ def tile_bag_lstm_pa_kernel(tc, x, h_prev, c_prev, is_rnn, W_words, W_scales, b,
         load_gate_scales(GATE_O)
         load_gate_words(GATE_O, 0)
         load_gate_words(GATE_O, 1)
+        nc.sync.dma_start(
+            out=bias_all[GATE_O][:], in_=b[GATE_O * HIDDEN : (GATE_O + 1) * HIDDEN].partition_broadcast(P)
+        )
 
-        bias_all = [
-            keep_pool.tile([P, HIDDEN], BF16, align_bytes=ALIGN, name="bias_all_%d" % gate) for gate in range(GATES)
-        ]
         xq_codes = [
             keep_pool.tile([P, K_GROUPS, P], U32, align_bytes=ALIGN, name="xq_codes_%d" % tile_index)
             for tile_index in range(ROW_TILES)
@@ -193,7 +196,6 @@ def tile_bag_lstm_pa_kernel(tc, x, h_prev, c_prev, is_rnn, W_words, W_scales, b,
         flip_rows(1)
         quantise_rows(0)
         spread_bias(GATE_G)
-        spread_bias(GATE_O)
         flip_rows(2)
         quantise_rows(1)
         flip_rows(3)

@@ -45,14 +45,16 @@ def tile_bag_lstm_pa_kernel(tc, x, h_prev, c_prev, is_rnn, W_words, W_scales, b,
         psum = pools.enter_context(tc.psum_pool(name="psum", bufs=8))
         pools.enter_context(tc.manual_schedule())
 
+        bias_landed = keep_pool.tile([P, N_TILE], BF16, align_bytes=ALIGN)
+        nc.sync.dma_start(
+            out=bias_landed[0 : GATES * HALVES, :], in_=b.rearrange("(c n) -> c n", n=N_TILE)
+        )
         bias_rows = keep_pool.tile([P, N_TILE], BF16, align_bytes=ALIGN)
         nc.gpsimd.memset(bias_rows[:].bitcast(F32), 0.0)
-        nc.sync.dma_start(
-            out=bias_rows[0 : GATES * HALVES, :], in_=b.rearrange("(c n) -> c n", n=N_TILE)
-        )
+        m_landed = keep_pool.tile([P, P], BF16, align_bytes=ALIGN)
+        nc.sync.dma_start(out=m_landed[0:ROW_TILES, :], in_=is_rnn.rearrange("(t p) o -> t (p o)", p=P))
         m_rows = keep_pool.tile([P, P], BF16, align_bytes=ALIGN)
         nc.gpsimd.memset(m_rows[:].bitcast(F32), 0.0)
-        nc.sync.dma_start(out=m_rows[0:ROW_TILES, :], in_=is_rnn.rearrange("(t p) o -> t (p o)", p=P))
         warm = keep_pool.tile([P, 1], F32, align_bytes=ALIGN)
         nc.vector.memset(warm[:], 0.0)
         nc.scalar.activation(out=warm[:], in_=warm[:], func=ACT.Sigmoid)
@@ -76,6 +78,9 @@ def tile_bag_lstm_pa_kernel(tc, x, h_prev, c_prev, is_rnn, W_words, W_scales, b,
         ]
         for gate in GATE_ORDER:
             nc.vector.memset(w_scales[gate][:].bitcast(I32), 0)
+            if gate == GATE_ORDER[0]:
+                nc.vector.tensor_copy(out=bias_rows[0 : GATES * HALVES, :], in_=bias_landed[0 : GATES * HALVES, :])
+                nc.vector.tensor_copy(out=m_rows[0:ROW_TILES, :], in_=m_landed[0:ROW_TILES, :])
 
         raw = {}
 

@@ -49,17 +49,29 @@ def tile_bag_lstm_pa_kernel(tc, x, h_prev, c_prev, is_rnn, W_words, W_scales, b,
         nc.sync.dma_start(
             out=bias_landed[0 : GATES * HALVES, :], in_=b.rearrange("(c n) -> c n", n=N_TILE)
         )
+        f_scales = [
+            keep_pool.tile([P, K_GROUPS, N_TILE], U8, align_bytes=ALIGN, name="f_scales_%d" % half)
+            for half in range(HALVES)
+        ]
+        nc.gpsimd.memset(f_scales[0][:].bitcast(I32), 0)
         bias_rows = keep_pool.tile([P, N_TILE], BF16, align_bytes=ALIGN)
         nc.gpsimd.memset(bias_rows[:].bitcast(F32), 0.0)
         m_landed = keep_pool.tile([P, P], BF16, align_bytes=ALIGN)
         nc.sync.dma_start(out=m_landed[0:ROW_TILES, :], in_=is_rnn.rearrange("(t p) o -> t (p o)", p=P))
         m_rows = keep_pool.tile([P, P], BF16, align_bytes=ALIGN)
         nc.gpsimd.memset(m_rows[:].bitcast(F32), 0.0)
+        w_scales = {
+            gate: keep_pool.tile([P, K_GROUPS, HIDDEN], U8, align_bytes=ALIGN, name="w_scales_%d" % gate)
+            for gate in GATE_ORDER[1:]
+        }
         warm = keep_pool.tile([P, 1], F32, align_bytes=ALIGN)
         nc.vector.memset(warm[:], 0.0)
         nc.scalar.activation(out=warm[:], in_=warm[:], func=ACT.Sigmoid)
         zeros = keep_pool.tile([P, N_TILE], BF16, align_bytes=ALIGN)
         nc.vector.memset(zeros[:].bitcast(I32), 0)
+        nc.vector.tensor_copy(out=bias_rows[0 : GATES * HALVES, :], in_=bias_landed[0 : GATES * HALVES, :])
+        nc.vector.tensor_copy(out=m_rows[0:ROW_TILES, :], in_=m_landed[0:ROW_TILES, :])
+        nc.vector.memset(f_scales[1][:].bitcast(I32), 0)
 
         ident_bf16 = keep_pool.tile([P, P], BF16, align_bytes=ALIGN)
         make_identity(nc, ident_bf16[:])
@@ -72,15 +84,8 @@ def tile_bag_lstm_pa_kernel(tc, x, h_prev, c_prev, is_rnn, W_words, W_scales, b,
                 w_words[(gate, half)] = keep_pool.tile(
                     [P, K_GROUPS, 2 * N_TILE], U8, align_bytes=ALIGN, name="w_words_%d_%d" % (gate, half)
                 )
-        w_scales = [
-            keep_pool.tile([P, K_GROUPS, HIDDEN], U8, align_bytes=ALIGN, name="w_scales_%d" % gate)
-            for gate in range(GATES)
-        ]
-        for gate in GATE_ORDER:
-            nc.vector.memset(w_scales[gate][:].bitcast(I32), 0)
-            if gate == GATE_ORDER[0]:
-                nc.vector.tensor_copy(out=bias_rows[0 : GATES * HALVES, :], in_=bias_landed[0 : GATES * HALVES, :])
-                nc.vector.tensor_copy(out=m_rows[0:ROW_TILES, :], in_=m_landed[0:ROW_TILES, :])
+        for gate in GATE_ORDER[1:]:
+            nc.gpsimd.memset(w_scales[gate][:].bitcast(I32), 0)
 
         raw = {}
 
@@ -93,13 +98,19 @@ def tile_bag_lstm_pa_kernel(tc, x, h_prev, c_prev, is_rnn, W_words, W_scales, b,
                 nc.sync.dma_start(out=raw_tile[:], in_=source[rows, :])
                 raw[(tile_index, source_index)] = raw_tile
 
-        def load_gate_scales(gate):
+        def load_scales(plane, first, width):
             scale_rows = W_scales.rearrange("g q n -> q g n")
             for r in range(4):
                 nc.sync.dma_start(
-                    out=w_scales[gate][r:P:32, :, :].bitcast(I32),
-                    in_=scale_rows[r:SCALE_ROWS:4, :, gate * HIDDEN : (gate + 1) * HIDDEN].bitcast(I32),
+                    out=plane[r:P:32, :, :].bitcast(I32),
+                    in_=scale_rows[r:SCALE_ROWS:4, :, first : first + width].bitcast(I32),
                 )
+
+        def load_gate_scales(gate):
+            load_scales(w_scales[gate], gate * HIDDEN, HIDDEN)
+
+        def load_f_scales(half):
+            load_scales(f_scales[half], GATE_F * HIDDEN + half * N_TILE, N_TILE)
 
         def load_gate_words(gate, half):
             first = 2 * (gate * HIDDEN + half * N_TILE)
@@ -122,17 +133,20 @@ def tile_bag_lstm_pa_kernel(tc, x, h_prev, c_prev, is_rnn, W_words, W_scales, b,
         bias_all = [
             keep_pool.tile([P, HIDDEN], BF16, align_bytes=ALIGN, name="bias_all_%d" % gate) for gate in range(GATES)
         ]
-        for tile_index in range(ROW_TILES):
-            load_rows(tile_index)
-        load_gate_scales(GATE_F)
+        load_rows(0)
+        load_f_scales(0)
+        load_rows(1)
         load_gate_words(GATE_F, 0)
-        load_c_old(0)
+        load_rows(2)
+        load_rows(3)
+        load_f_scales(1)
         load_gate_words(GATE_F, 1)
-        load_c_old(1)
+        load_c_old(0)
         load_gate_scales(GATE_I)
-        load_gate_words(GATE_I, 0)
         load_gate_scales(GATE_G)
+        load_gate_words(GATE_I, 0)
         load_gate_words(GATE_G, 0)
+        load_c_old(1)
         load_gate_words(GATE_I, 1)
         load_gate_words(GATE_G, 1)
         load_gate_scales(GATE_O)
@@ -162,7 +176,7 @@ def tile_bag_lstm_pa_kernel(tc, x, h_prev, c_prev, is_rnn, W_words, W_scales, b,
                     start=True,
                     stop=True,
                 )
-            nc.scalar.copy(out=bias_all[gate][:], in_=spread[:])
+            return lambda: nc.scalar.copy(out=bias_all[gate][:], in_=spread[:])
 
         grouped = {}
 
@@ -195,17 +209,10 @@ def tile_bag_lstm_pa_kernel(tc, x, h_prev, c_prev, is_rnn, W_words, W_scales, b,
         warm_bank = psum.tile([P, N_TILE], F32, tag="bank")
         for step in range(WARM_UP_MATMULS):
             nc.tensor.matmul(out=warm_bank[:], lhsT=zeros[:, 0:P], rhs=zeros[:], start=True, stop=True)
-        spread_bias(GATE_F)
-        spread_bias(GATE_I)
+        copy_bias_f = spread_bias(GATE_F)
         flip_rows(0)
-        flip_rows(1)
-        quantise_rows(0)
-        spread_bias(GATE_G)
-        flip_rows(2)
-        quantise_rows(1)
-        flip_rows(3)
-        quantise_rows(2)
-        quantise_rows(3)
+        copy_bias_f()
+        copy_bias_i = spread_bias(GATE_I)
 
         m_flipped = psum.tile([P, P], BF16, tag="bank")
         nc.tensor.transpose(m_flipped[:], m_rows[:], ident_bf16[:])
@@ -215,6 +222,12 @@ def tile_bag_lstm_pa_kernel(tc, x, h_prev, c_prev, is_rnn, W_words, W_scales, b,
         nc.vector.tensor_scalar(
             out=one_minus_m[:], in0=m_col[:], scalar1=-1.0, scalar2=1.0, op0=ALU.mult, op1=ALU.add
         )
+        flip_rows(1)
+        copy_bias_i()
+        quantise_rows(0)
+        copy_bias_g = spread_bias(GATE_G)
+        copy_bias_g()
+        quantise_rows(1)
 
         in_gate = {}
         new_part = {}
@@ -237,6 +250,10 @@ def tile_bag_lstm_pa_kernel(tc, x, h_prev, c_prev, is_rnn, W_words, W_scales, b,
         def preactivation(gate, cell, first, width):
             tile_index, half = cell
             cols = slice(half * N_TILE + first, half * N_TILE + first + width)
+            if gate == GATE_F:
+                planes, plane_first = f_scales[half], first
+            else:
+                planes, plane_first = w_scales[gate], half * N_TILE + first
             acc = psum.tile([P, width], F32, tag="bank")
             for group in range(K_GROUPS):
                 nc.tensor.matmul_mx(
@@ -244,7 +261,7 @@ def tile_bag_lstm_pa_kernel(tc, x, h_prev, c_prev, is_rnn, W_words, W_scales, b,
                     lhsT=xq_codes[tile_index][:, group, :].bitcast(FP8X4),
                     lhsT_scale=xq_scales[tile_index][:, group, :],
                     rhs=w_words[(gate, half)][:, group, 2 * first : 2 * (first + width)].bitcast(FP4X4),
-                    rhs_scale=w_scales[gate][:, group, cols],
+                    rhs_scale=planes[:, group, plane_first : plane_first + width],
                     start=(group == 0),
                     stop=(group == K_GROUPS - 1),
                 )
@@ -332,9 +349,15 @@ def tile_bag_lstm_pa_kernel(tc, x, h_prev, c_prev, is_rnn, W_words, W_scales, b,
         postponed = []
         for slot, (gate, cell, first, width) in enumerate(order):
             unit(slot, gate, cell, first, width)
+            if slot == 0:
+                flip_rows(2)
+                flip_rows(3)
             if width == N_TILE:
                 for action in later.get(slot, []):
                     action()
+                if slot == 0:
+                    quantise_rows(2)
+                    quantise_rows(3)
             else:
                 postponed.extend(later.get(slot, []))
         for action in postponed:

@@ -30,7 +30,7 @@ SCALE_ROWS = K_PASS // 32
 WARM_UP_MATMULS = 3
 ALIGN = 256
 NARROW = 128
-NARROW_UNITS = 1
+MIDDLE = 256
 
 FLOPS = 2 * BATCH * 2 * HIDDEN * GATES * HIDDEN
 
@@ -41,7 +41,8 @@ def tile_bag_lstm_pa_kernel(tc, x, h_prev, c_prev, is_rnn, W_words, W_scales, b,
         keep_pool = pools.enter_context(tc.tile_pool(name="keep", bufs=1))
         stage = pools.enter_context(tc.tile_pool(name="stage", bufs=3))
         work = pools.enter_context(tc.tile_pool(name="work", bufs=4))
-        pieces = pools.enter_context(tc.tile_pool(name="pieces", bufs=NARROW_UNITS * N_TILE // NARROW))
+        pieces = pools.enter_context(tc.tile_pool(name="pieces", bufs=N_TILE // NARROW))
+        middles = pools.enter_context(tc.tile_pool(name="middles", bufs=N_TILE // MIDDLE))
         psum = pools.enter_context(tc.psum_pool(name="psum", bufs=8))
         pools.enter_context(tc.manual_schedule())
 
@@ -212,6 +213,7 @@ def tile_bag_lstm_pa_kernel(tc, x, h_prev, c_prev, is_rnn, W_words, W_scales, b,
         copy_bias_f = spread_bias(GATE_F)
         flip_rows(0)
         copy_bias_f()
+        quantise_rows(0)
         copy_bias_i = spread_bias(GATE_I)
 
         m_flipped = psum.tile([P, P], BF16, tag="bank")
@@ -224,7 +226,6 @@ def tile_bag_lstm_pa_kernel(tc, x, h_prev, c_prev, is_rnn, W_words, W_scales, b,
         )
         flip_rows(1)
         copy_bias_i()
-        quantise_rows(0)
         copy_bias_g = spread_bias(GATE_G)
         copy_bias_g()
         quantise_rows(1)
@@ -245,7 +246,7 @@ def tile_bag_lstm_pa_kernel(tc, x, h_prev, c_prev, is_rnn, W_words, W_scales, b,
             return out[tile_index * P : (tile_index + 1) * P, half * N_TILE + first : half * N_TILE + first + width]
 
         def pool_of(width):
-            return work if width == N_TILE else pieces
+            return {N_TILE: work, MIDDLE: middles, NARROW: pieces}[width]
 
         def preactivation(gate, cell, first, width):
             tile_index, half = cell
@@ -255,16 +256,18 @@ def tile_bag_lstm_pa_kernel(tc, x, h_prev, c_prev, is_rnn, W_words, W_scales, b,
             else:
                 planes, plane_first = w_scales[gate], half * N_TILE + first
             acc = psum.tile([P, width], F32, tag="bank")
-            for group in range(K_GROUPS):
-                nc.tensor.matmul_mx(
-                    out=acc[:],
-                    lhsT=xq_codes[tile_index][:, group, :].bitcast(FP8X4),
-                    lhsT_scale=xq_scales[tile_index][:, group, :],
-                    rhs=w_words[(gate, half)][:, group, 2 * first : 2 * (first + width)].bitcast(FP4X4),
-                    rhs_scale=planes[:, group, plane_first : plane_first + width],
-                    start=(group == 0),
-                    stop=(group == K_GROUPS - 1),
-                )
+            n_pass = width if width == N_TILE else NARROW
+            for n in range(0, width, n_pass):
+                for group in range(K_GROUPS):
+                    nc.tensor.matmul_mx(
+                        out=acc[:, n : n + n_pass],
+                        lhsT=xq_codes[tile_index][:, group, :].bitcast(FP8X4),
+                        lhsT_scale=xq_scales[tile_index][:, group, :],
+                        rhs=w_words[(gate, half)][:, group, 2 * (first + n) : 2 * (first + n + n_pass)].bitcast(FP4X4),
+                        rhs_scale=planes[:, group, plane_first + n : plane_first + n + n_pass],
+                        start=(group == 0),
+                        stop=(group == K_GROUPS - 1),
+                    )
             z = pool_of(width).tile([P, width], F32, align_bytes=ALIGN, name="z")
             nc.vector.tensor_tensor(out=z[:], in0=acc[:], in1=bias_all[gate][:, cols], op=ALU.add)
             return z
@@ -280,11 +283,10 @@ def tile_bag_lstm_pa_kernel(tc, x, h_prev, c_prev, is_rnn, W_words, W_scales, b,
 
         def old_product(cell, forget):
             tile_index, half = cell
-            retain = work.tile([P, N_TILE], F32, align_bytes=ALIGN)
-            blend(retain[:], forget[:], tile_index)
+            blend(forget[:], forget[:], tile_index)
             old_part[cell] = cell_tile("old_part", cell)
             nc.gpsimd.tensor_tensor(
-                out=old_part[cell][:], in0=retain[:], in1=c_old[half][:, tile_index, :], op=ALU.mult
+                out=old_part[cell][:], in0=forget[:], in1=c_old[half][:, tile_index, :], op=ALU.mult
             )
 
         def new_product(cell, candidate):
@@ -342,9 +344,9 @@ def tile_bag_lstm_pa_kernel(tc, x, h_prev, c_prev, is_rnn, W_words, W_scales, b,
         for cell in cells:
             order.append((GATE_I, cell, 0, N_TILE))
             order.append((GATE_G, cell, 0, N_TILE))
-        order.extend([(GATE_O, cell, 0, N_TILE) for cell in cells[0 : len(cells) - NARROW_UNITS]])
-        for cell in cells[len(cells) - NARROW_UNITS :]:
-            order.extend([(GATE_O, cell, first, NARROW) for first in range(0, N_TILE, NARROW)])
+        order.extend([(GATE_O, cell, 0, N_TILE) for cell in cells[:-2]])
+        order.extend([(GATE_O, cells[-2], first, MIDDLE) for first in range(0, N_TILE, MIDDLE)])
+        order.extend([(GATE_O, cells[-1], first, NARROW) for first in range(0, N_TILE, NARROW)])
 
         postponed = []
         for slot, (gate, cell, first, width) in enumerate(order):
@@ -352,7 +354,7 @@ def tile_bag_lstm_pa_kernel(tc, x, h_prev, c_prev, is_rnn, W_words, W_scales, b,
             if slot == 0:
                 flip_rows(2)
                 flip_rows(3)
-            if width == N_TILE:
+            if width != NARROW:
                 for action in later.get(slot, []):
                     action()
                 if slot == 0:

@@ -309,7 +309,8 @@ def tile_bag_lstm_pa_kernel(tc, x, h_prev, c_prev, is_rnn, W_words, W_scales, b,
         def store_output(cell, first, width, out_gate):
             tile_index = cell[0]
             o_new = pool_of(width).tile([P, width], F32, align_bytes=ALIGN, name="o_new")
-            nc.vector.tensor_scalar(
+            blend_engine = nc.gpsimd if width == N_TILE else nc.vector
+            blend_engine.tensor_scalar(
                 out=o_new[:],
                 in0=out_gate[:],
                 scalar1=m_col[:, tile_index : tile_index + 1],
@@ -336,7 +337,7 @@ def tile_bag_lstm_pa_kernel(tc, x, h_prev, c_prev, is_rnn, W_words, W_scales, b,
             else:
                 out_gate = pool_of(width).tile([P, width], F32, align_bytes=ALIGN, name="out_gate")
                 nc.scalar.activation(out=out_gate[:], in_=z[:], func=ACT.Sigmoid)
-                write_later(slot + 2 * N_TILE // width, lambda: store_output(cell, first, width, out_gate))
+                write_later(slot + (1 if width == N_TILE else 2 * N_TILE // width), lambda: store_output(cell, first, width, out_gate))
 
         order = []
         cells = [(tile_index, half) for half in range(HALVES) for tile_index in range(ROW_TILES)]

from contextlib import ExitStack

import concourse.mybir as mybir
from concourse.masks import make_identity

F32 = mybir.dt.float32
BF16 = mybir.dt.bfloat16
I32 = mybir.dt.int32
U8 = mybir.dt.uint8
U32 = mybir.dt.uint32
FP8X4 = mybir.dt.float8_e4m3fn_x4
FP4X4 = mybir.dt.float4_e2m1fn_x4
ACT = mybir.ActivationFunctionType
ALU = mybir.AluOpType

P = 128
BATCH = 512
HIDDEN = 1024
PACK = 4
K_PASS = P * PACK
K_GROUPS = 2 * HIDDEN // K_PASS
SOURCE_GROUPS = HIDDEN // K_PASS
ROW_TILES = BATCH // P
N_TILE = 512
HALVES = HIDDEN // N_TILE
GATE_I, GATE_F, GATE_G, GATE_O = 0, 1, 2, 3
GATES = 4
GATE_ORDER = (GATE_F, GATE_I, GATE_G, GATE_O)
SCALE_ROWS = K_PASS // 32
WARM_UP_MATMULS = 3
ALIGN = 256
NARROW = 128
MIDDLE = 256

FLOPS = 2 * BATCH * 2 * HIDDEN * GATES * HIDDEN


def tile_bag_lstm_pa_kernel(tc, x, h_prev, c_prev, is_rnn, W_words, W_scales, b, out_0, out_1):
    nc = tc.nc
    with ExitStack() as pools:
        keep_pool = pools.enter_context(tc.tile_pool(name="keep", bufs=1))
        stage = pools.enter_context(tc.tile_pool(name="stage", bufs=3))
        work = pools.enter_context(tc.tile_pool(name="work", bufs=4))
        pieces = pools.enter_context(tc.tile_pool(name="pieces", bufs=N_TILE // NARROW))
        middles = pools.enter_context(tc.tile_pool(name="middles", bufs=N_TILE // MIDDLE))
        psum = pools.enter_context(tc.psum_pool(name="psum", bufs=8))
        pools.enter_context(tc.manual_schedule())

        bias_landed = keep_pool.tile([P, N_TILE], BF16, align_bytes=ALIGN)
        nc.sync.dma_start(
            out=bias_landed[0 : GATES * HALVES, :], in_=b.rearrange("(c n) -> c n", n=N_TILE)
        )
        f_scales = [
            keep_pool.tile([P, K_GROUPS, N_TILE], U8, align_bytes=ALIGN, name="f_scales_%d" % half)
            for half in range(HALVES)
        ]
        nc.gpsimd.memset(f_scales[0][:].bitcast(I32), 0)
        bias_rows = keep_pool.tile([P, N_TILE], BF16, align_bytes=ALIGN)
        nc.gpsimd.memset(bias_rows[:].bitcast(F32), 0.0)
        m_landed = keep_pool.tile([P, P], BF16, align_bytes=ALIGN)
        nc.sync.dma_start(out=m_landed[0:ROW_TILES, :], in_=is_rnn.rearrange("(t p) o -> t (p o)", p=P))
        m_rows = keep_pool.tile([P, P], BF16, align_bytes=ALIGN)
        nc.gpsimd.memset(m_rows[:].bitcast(F32), 0.0)
        w_scales = {
            gate: keep_pool.tile([P, K_GROUPS, HIDDEN], U8, align_bytes=ALIGN, name="w_scales_%d" % gate)
            for gate in GATE_ORDER[1:]
        }
        warm = keep_pool.tile([P, 1], F32, align_bytes=ALIGN)
        nc.vector.memset(warm[:], 0.0)
        nc.scalar.activation(out=warm[:], in_=warm[:], func=ACT.Sigmoid)
        zeros = keep_pool.tile([P, N_TILE], BF16, align_bytes=ALIGN)
        nc.vector.memset(zeros[:].bitcast(I32), 0)
        nc.vector.tensor_copy(out=bias_rows[0 : GATES * HALVES, :], in_=bias_landed[0 : GATES * HALVES, :])
        nc.vector.tensor_copy(out=m_rows[0:ROW_TILES, :], in_=m_landed[0:ROW_TILES, :])
        nc.vector.memset(f_scales[1][:].bitcast(I32), 0)

        ident_bf16 = keep_pool.tile([P, P], BF16, align_bytes=ALIGN)
        make_identity(nc, ident_bf16[:])
        ident_f32 = keep_pool.tile([P, P], F32, align_bytes=ALIGN)
        make_identity(nc, ident_f32[:])

        w_words = {}
        for gate in range(GATES):
            for half in range(HALVES):
                w_words[(gate, half)] = keep_pool.tile(
                    [P, K_GROUPS, 2 * N_TILE], U8, align_bytes=ALIGN, name="w_words_%d_%d" % (gate, half)
                )
        for gate in GATE_ORDER[1:]:
            nc.gpsimd.memset(w_scales[gate][:].bitcast(I32), 0)

        raw = {}

        def load_rows(tile_index):
            rows = slice(tile_index * P, (tile_index + 1) * P)
            for source_index, source in enumerate((x, h_prev)):
                raw_tile = keep_pool.tile(
                    [P, HIDDEN], BF16, align_bytes=ALIGN, name="raw_%d_%d" % (tile_index, source_index)
                )
                nc.sync.dma_start(out=raw_tile[:], in_=source[rows, :])
                raw[(tile_index, source_index)] = raw_tile

        def load_scales(plane, first, width):
            scale_rows = W_scales.rearrange("g q n -> q g n")
            for r in range(4):
                nc.sync.dma_start(
                    out=plane[r:P:32, :, :].bitcast(I32),
                    in_=scale_rows[r:SCALE_ROWS:4, :, first : first + width].bitcast(I32),
                )

        def load_gate_scales(gate):
            load_scales(w_scales[gate], gate * HIDDEN, HIDDEN)

        def load_f_scales(half):
            load_scales(f_scales[half], GATE_F * HIDDEN + half * N_TILE, N_TILE)

        def load_gate_words(gate, half):
            first = 2 * (gate * HIDDEN + half * N_TILE)
            nc.sync.dma_start(
                out=w_words[(gate, half)][:].bitcast(I32),
                in_=W_words[:, :, first : first + 2 * N_TILE].bitcast(I32).rearrange("g p n -> p g n"),
            )

        c_old = [
            keep_pool.tile([P, ROW_TILES, N_TILE], BF16, align_bytes=ALIGN, name="c_old_%d" % half)
            for half in range(HALVES)
        ]

        def load_c_old(half):
            nc.sync.dma_start(
                out=c_old[half][:],
                in_=c_prev.rearrange("(t p) c -> p t c", p=P)[:, :, half * N_TILE : (half + 1) * N_TILE],
            )

        bias_all = [
            keep_pool.tile([P, HIDDEN], BF16, align_bytes=ALIGN, name="bias_all_%d" % gate) for gate in range(GATES)
        ]
        load_rows(0)
        load_f_scales(0)
        load_rows(1)
        load_gate_words(GATE_F, 0)
        load_rows(2)
        load_rows(3)
        load_f_scales(1)
        load_gate_words(GATE_F, 1)
        load_c_old(0)
        load_gate_scales(GATE_I)
        load_gate_scales(GATE_G)
        load_gate_words(GATE_I, 0)
        load_gate_words(GATE_G, 0)
        load_c_old(1)
        load_gate_words(GATE_I, 1)
        load_gate_words(GATE_G, 1)
        load_gate_scales(GATE_O)
        load_gate_words(GATE_O, 0)
        load_gate_words(GATE_O, 1)
        nc.sync.dma_start(
            out=bias_all[GATE_O][:], in_=b[GATE_O * HIDDEN : (GATE_O + 1) * HIDDEN].partition_broadcast(P)
        )

        xq_codes = [
            keep_pool.tile([P, K_GROUPS, P], U32, align_bytes=ALIGN, name="xq_codes_%d" % tile_index)
            for tile_index in range(ROW_TILES)
        ]
        xq_scales = [
            keep_pool.tile([P, K_GROUPS, P], U8, align_bytes=ALIGN, name="xq_scales_%d" % tile_index)
            for tile_index in range(ROW_TILES)
        ]

        def spread_bias(gate):
            spread = psum.tile([P, HIDDEN], BF16, tag="bank")
            for half in range(HALVES):
                c = gate * HALVES + half
                nc.tensor.matmul(
                    out=spread[:, half * N_TILE : (half + 1) * N_TILE],
                    lhsT=ident_bf16[:, c : c + 1].to_broadcast([P, P]),
                    rhs=bias_rows[:],
                    start=True,
                    stop=True,
                )
            return lambda: nc.scalar.copy(out=bias_all[gate][:], in_=spread[:])

        grouped = {}

        def flip_rows(tile_index):
            grouped[tile_index] = stage.tile([P, K_GROUPS, P, PACK], BF16, align_bytes=ALIGN, name="grouped")
            for source_index in range(2):
                words = raw[(tile_index, source_index)][:].bitcast(F32)
                flipped = psum.tile([P, SOURCE_GROUPS, 2, P], F32, tag="bank")
                for group in range(SOURCE_GROUPS):
                    for u in range(2):
                        nc.tensor.transpose(
                            flipped[:, group, u, :],
                            words[:, 256 * group + u : 256 * (group + 1) : 2],
                            ident_f32[:],
                        )
                groups = slice(source_index * SOURCE_GROUPS, (source_index + 1) * SOURCE_GROUPS)
                copy_out = nc.vector.tensor_copy if source_index == 0 else nc.scalar.copy
                copy_out(
                    out=grouped[tile_index][:, groups, :, :].bitcast(F32),
                    in_=flipped[:].rearrange("p g u r -> p g r u"),
                )

        def quantise_rows(tile_index):
            nc.vector.quantize_mx(
                out=xq_codes[tile_index][:].rearrange("p g r -> p (g r)").bitcast(FP8X4),
                scales=xq_scales[tile_index][:].rearrange("p g r -> p (g r)"),
                in_=grouped[tile_index][:].rearrange("p g r t -> p (g r t)"),
            )

        warm_bank = psum.tile([P, N_TILE], F32, tag="bank")
        for step in range(WARM_UP_MATMULS):
            nc.tensor.matmul(out=warm_bank[:], lhsT=zeros[:, 0:P], rhs=zeros[:], start=True, stop=True)
        copy_bias_f = spread_bias(GATE_F)
        flip_rows(0)
        copy_bias_f()
        quantise_rows(0)
        copy_bias_i = spread_bias(GATE_I)

        m_flipped = psum.tile([P, P], BF16, tag="bank")
        nc.tensor.transpose(m_flipped[:], m_rows[:], ident_bf16[:])
        m_col = keep_pool.tile([P, ROW_TILES], F32, align_bytes=ALIGN)
        nc.vector.tensor_copy(out=m_col[:], in_=m_flipped[:, 0:ROW_TILES])
        one_minus_m = keep_pool.tile([P, ROW_TILES], F32, align_bytes=ALIGN)
        nc.vector.tensor_scalar(
            out=one_minus_m[:], in0=m_col[:], scalar1=-1.0, scalar2=1.0, op0=ALU.mult, op1=ALU.add
        )
        flip_rows(1)
        copy_bias_i()
        copy_bias_g = spread_bias(GATE_G)
        copy_bias_g()
        quantise_rows(1)

        in_gate = {}
        new_part = {}
        old_part = {}
        later = {}

        def write_later(slot, action):
            later.setdefault(slot, []).append(action)

        def cell_tile(label, cell):
            return keep_pool.tile([P, N_TILE], F32, align_bytes=ALIGN, name="%s_%d_%d" % (label, cell[0], cell[1]))

        def out_view(out, cell, first=0, width=N_TILE):
            tile_index, half = cell
            return out[tile_index * P : (tile_index + 1) * P, half * N_TILE + first : half * N_TILE + first + width]

        def pool_of(width):
            return {N_TILE: work, MIDDLE: middles, NARROW: pieces}[width]

        def preactivation(gate, cell, first, width):
            tile_index, half = cell
            cols = slice(half * N_TILE + first, half * N_TILE + first + width)
            if gate == GATE_F:
                planes, plane_first = f_scales[half], first
            else:
                planes, plane_first = w_scales[gate], half * N_TILE + first
            acc = psum.tile([P, width], F32, tag="bank")
            n_pass = width if width == N_TILE else NARROW
            for n in range(0, width, n_pass):
                for group in range(K_GROUPS):
                    nc.tensor.matmul_mx(
                        out=acc[:, n : n + n_pass],
                        lhsT=xq_codes[tile_index][:, group, :].bitcast(FP8X4),
                        lhsT_scale=xq_scales[tile_index][:, group, :],
                        rhs=w_words[(gate, half)][:, group, 2 * (first + n) : 2 * (first + n + n_pass)].bitcast(FP4X4),
                        rhs_scale=planes[:, group, plane_first + n : plane_first + n + n_pass],
                        start=(group == 0),
                        stop=(group == K_GROUPS - 1),
                    )
            z = pool_of(width).tile([P, width], F32, align_bytes=ALIGN, name="z")
            nc.vector.tensor_tensor(out=z[:], in0=acc[:], in1=bias_all[gate][:, cols], op=ALU.add)
            return z

        def blend(out, gate_values, tile_index):
            nc.scalar.activation(
                out=out,
                in_=gate_values,
                func=ACT.Identity,
                scale=m_col[:, tile_index : tile_index + 1],
                bias=one_minus_m[:, tile_index : tile_index + 1],
            )

        def old_product(cell, forget):
            tile_index, half = cell
            blend(forget[:], forget[:], tile_index)
            old_part[cell] = cell_tile("old_part", cell)
            nc.gpsimd.tensor_tensor(
                out=old_part[cell][:], in0=forget[:], in1=c_old[half][:, tile_index, :], op=ALU.mult
            )

        def new_product(cell, candidate):
            tile_index = cell[0]
            new_part[cell] = cell_tile("new_part", cell)
            nc.vector.scalar_tensor_tensor(
                out=new_part[cell][:],
                in0=in_gate[cell][:],
                scalar=m_col[:, tile_index : tile_index + 1],
                in1=candidate[:],
                op0=ALU.mult,
                op1=ALU.mult,
            )

        def store_cell_state(cell):
            c_new = work.tile([P, N_TILE], F32, align_bytes=ALIGN)
            nc.vector.tensor_tensor(out=c_new[:], in0=new_part[cell][:], in1=old_part[cell][:], op=ALU.add)
            nc.sync.dma_start(out=out_view(out_0, cell), in_=c_new[:])

        def store_output(cell, first, width, out_gate):
            tile_index = cell[0]
            o_new = pool_of(width).tile([P, width], F32, align_bytes=ALIGN, name="o_new")
            blend_engine = nc.gpsimd if width == N_TILE else nc.vector
            blend_engine.tensor_scalar(
                out=o_new[:],
                in0=out_gate[:],
                scalar1=m_col[:, tile_index : tile_index + 1],
                scalar2=one_minus_m[:, tile_index : tile_index + 1],
                op0=ALU.mult,
                op1=ALU.add,
            )
            nc.sync.dma_start(out=out_view(out_1, cell, first, width), in_=o_new[:])

        def unit(slot, gate, cell, first, width):
            z = preactivation(gate, cell, first, width)
            if gate == GATE_I:
                in_gate[cell] = cell_tile("in_gate", cell)
                nc.scalar.activation(out=in_gate[cell][:], in_=z[:], func=ACT.Sigmoid)
            elif gate == GATE_F:
                forget = work.tile([P, N_TILE], F32, align_bytes=ALIGN)
                nc.scalar.activation(out=forget[:], in_=z[:], func=ACT.Sigmoid)
                write_later(slot + 1, lambda: old_product(cell, forget))
            elif gate == GATE_G:
                candidate = work.tile([P, N_TILE], F32, align_bytes=ALIGN)
                nc.scalar.activation(out=candidate[:], in_=z[:], func=ACT.Tanh)
                write_later(slot + 2, lambda: new_product(cell, candidate))
                write_later(slot + 3, lambda: store_cell_state(cell))
            else:
                out_gate = pool_of(width).tile([P, width], F32, align_bytes=ALIGN, name="out_gate")
                nc.scalar.activation(out=out_gate[:], in_=z[:], func=ACT.Sigmoid)
                write_later(slot + (1 if width == N_TILE else 2 * N_TILE // width), lambda: store_output(cell, first, width, out_gate))

        order = []
        cells = [(tile_index, half) for half in range(HALVES) for tile_index in range(ROW_TILES)]
        order.extend([(GATE_F, cell, 0, N_TILE) for cell in cells])
        for cell in cells:
            order.append((GATE_I, cell, 0, N_TILE))
            order.append((GATE_G, cell, 0, N_TILE))
        order.extend([(GATE_O, cell, 0, N_TILE) for cell in cells[:-2]])
        order.extend([(GATE_O, cells[-2], first, MIDDLE) for first in range(0, N_TILE, MIDDLE)])
        order.extend([(GATE_O, cells[-1], first, NARROW) for first in range(0, N_TILE, NARROW)])

        postponed = []
        for slot, (gate, cell, first, width) in enumerate(order):
            unit(slot, gate, cell, first, width)
            if slot == 0:
                flip_rows(2)
                flip_rows(3)
            if width != NARROW:
                for action in later.get(slot, []):
                    action()
                if slot == 0:
                    quantise_rows(2)
                    quantise_rows(3)
            else:
                postponed.extend(later.get(slot, []))
        for action in postponed:
            action()
        for slot in range(len(order), len(order) + 2 * N_TILE // NARROW + 1):
            for action in later.get(slot, []):
                action()
